import numpy as np
import ml_dtypes


def mxq(x, axis, fmt="e4m3"):
    dtype, down = {"e4m3": (ml_dtypes.float8_e4m3fn, 7), "e5m2": (ml_dtypes.float8_e5m2, 14)}[fmt]
    v = np.moveaxis(np.asarray(x, np.float32).astype(ml_dtypes.bfloat16).astype(np.float64), axis, -1)
    blocks = v.reshape(v.shape[:-1] + (-1, 32))
    amax = np.abs(blocks).max(-1, keepdims=True)
    byte = np.maximum(np.where(amax > 0, np.frexp(amax)[1] - 1 + 127, 0) - down, 1)
    scale = np.exp2(byte - 127.0)
    codes = (blocks / scale).astype(np.float32).astype(dtype).astype(np.float64)
    return np.moveaxis((codes * scale).reshape(v.shape), -1, axis)


WIDE = False


def mx_kscale(k):
    if not WIDE:
        return np.ones(k)
    levels = np.array([10, -10, 5, -5, 0])
    if k % 512:
        return np.exp2(np.random.permutation(np.resize(levels, k // 32))).repeat(32)
    a = np.empty((k // 512, 16))
    for p in range(k // 512):
        a[p, :8] = np.random.permutation(np.resize(levels, 8))
        for g in range(8):
            far = levels[np.abs(levels - a[p, g]) >= 10]
            a[p, g + 8] = far[np.random.randint(len(far))]
    return np.exp2(a.ravel()).repeat(32)


BF16 = ml_dtypes.bfloat16


def bf(x):
    return np.asarray(x, np.float32).astype(BF16)


def f64(x):
    return np.asarray(x).astype(np.float64)


N, T, D, B0, C, P0, V1, P1, V2 = 2, 128, 8192, 1022, 2, 512, 2048, 512, 1024
MU = 0.25
SIG = 2.0


def softmax(v):
    e = np.exp(v - v.max(-1, keepdims=True))
    return e / e.sum(-1, keepdims=True)


def setup_inputs():
    s, t = mx_kscale(D), mx_kscale(P0)
    hw = np.random.standard_normal((D, B0 + C)) * SIG / np.sqrt(D)
    hw[:, B0:] = hw[:, B0:] / SIG + (np.log(B0) + 0.5 * SIG * SIG) / (MU * D)
    return {"x": bf((np.random.standard_normal((N, T, D)) + MU) * s),
            "head_weight": bf(hw / s[:, None]),
            "tail_proj_0": bf(np.random.standard_normal((D, P0)) / np.sqrt(D) / s[:, None] * t),
            "tail_w_0": bf(np.random.standard_normal((P0, V1)) * SIG / np.sqrt(P0) / t[:, None])}


def reference(x, head_weight, tail_proj_0, tail_w_0):
    xq = mxq(f64(x), 2, "e4m3")
    head_sm = softmax(xq @ mxq(f64(head_weight), 0, "e4m3"))
    h = xq @ mxq(f64(tail_proj_0), 0, "e4m3")
    tail_sm = softmax(mxq(h, 2, "e4m3") @ mxq(f64(tail_w_0), 0, "e4m3"))
    probs = np.concatenate([head_sm[..., :B0], tail_sm * head_sm[..., B0:B0 + 1]], axis=-1)
    return probs, head_sm[..., B0 + 1:B0 + C]

@@ -1,0 +1,381 @@
+from contextlib import ExitStack
+
+import concourse.mybir as mybir
+from concourse.masks import make_identity
+
+F32 = mybir.dt.float32
+BF16 = mybir.dt.bfloat16
+U32 = mybir.dt.uint32
+U8 = mybir.dt.uint8
+FP8X4 = mybir.dt.float8_e4m3fn_x4
+EXP = mybir.ActivationFunctionType.Exp
+COPY = mybir.ActivationFunctionType.Copy
+MULT = mybir.AluOpType.mult
+MAX = mybir.AluOpType.max
+ALONG_ROW = mybir.AxisListType.X
+
+P = 128
+PACK = 4
+K_PASS = P * PACK
+BANK = 512
+
+TOKEN_TILES = 2
+TOKENS = TOKEN_TILES * P
+D = 8192
+PASSES = D // K_PASS
+HEAD = 1024
+HEAD_TOKENS = 1022
+PROJ = 512
+TAIL = 2048
+
+BLOCKS = 2
+CHUNK = BLOCKS * BANK
+X_PASSES = 4
+STORE_COLUMNS = 1024
+LAG = 2
+PIECE = 256
+RUN = 4
+
+FLOPS = 2 * TOKENS * D * (HEAD + PROJ) + 2 * TOKENS * PROJ * TAIL
+
+
+def tile_adaptiveinputsoftmax_pa_k_kernel(
+    tc, x, head_weight, tail_proj_0, tail_w_0, out_0, out_1
+):
+    nc = tc.nc
+    with ExitStack() as ctx:
+        keep = ctx.enter_context(tc.tile_pool(name="keep", bufs=1))
+        x_pool = ctx.enter_context(tc.tile_pool(name="x_pool", bufs=4))
+        x_grouped_pool = ctx.enter_context(tc.tile_pool(name="x_grouped_pool", bufs=2))
+        raw_pool = ctx.enter_context(tc.tile_pool(name="raw_pool", bufs=8))
+        grouped_pool = ctx.enter_context(tc.tile_pool(name="grouped_pool", bufs=LAG + 2))
+        codes_pool = ctx.enter_context(tc.tile_pool(name="codes_pool", bufs=3))
+        psum = ctx.enter_context(tc.psum_pool(name="psum", bufs=1))
+
+        def bank(index, name):
+            return psum.tile([P, BANK], F32, tag="bank%d" % index, name=name)[:]
+
+        identity = keep.tile([P, P], F32, name="identity")
+        make_identity(nc, identity[:])
+        zero = keep.tile([P, 1], F32, name="zero")
+        one = keep.tile([P, 1], F32, name="one")
+        nc.vector.memset(zero[:], 0.0)
+        nc.scalar.activation(out=one[:], in_=zero[:], func=EXP)
+        cluster1 = keep.tile([P, P], F32, name="cluster1")
+        nc.vector.memset(cluster1[:], 0.0)
+
+        x_codes = keep.tile([P, PASSES * TOKENS], U32, align_bytes=64, name="x_codes")
+        x_scales = keep.tile([P, PASSES * TOKENS], U8, align_bytes=64, name="x_scales")
+
+        def transpose_x(a):
+            columns = slice(X_PASSES * K_PASS * a, X_PASSES * K_PASS * (a + 1))
+            words = []
+            for m in range(TOKEN_TILES):
+                x_raw = x_pool.tile([P, X_PASSES * K_PASS], BF16, name="x_raw")
+                nc.sync.dma_start(out=x_raw[:], in_=x[m, :, columns])
+                words.append(
+                    x_raw[:].bitcast(F32).rearrange("r (g p u) -> r g u p", g=X_PASSES, u=2)
+                )
+            x_grouped = x_grouped_pool.tile(
+                [P, X_PASSES * TOKENS * PACK], BF16, align_bytes=64, name="x_grouped"
+            )
+            grouped_words = x_grouped[:].bitcast(F32).rearrange(
+                "p (g r u) -> p g r u", g=X_PASSES, u=2
+            )
+            for g in range(X_PASSES):
+                xt = bank(g, "xt").rearrange("p (u r) -> p u r", u=2)
+                for u in range(2):
+                    for m in range(TOKEN_TILES):
+                        nc.tensor.transpose(
+                            xt[:, u, P * m : P * (m + 1)], words[m][:, g, u, :], identity[:]
+                        )
+                nc.scalar.copy(out=grouped_words[:, g], in_=xt.rearrange("p u r -> p r u"))
+            return x_grouped
+
+        def quantise_x(a, x_grouped):
+            columns = slice(X_PASSES * TOKENS * a, X_PASSES * TOKENS * (a + 1))
+            nc.vector.quantize_mx(
+                out=x_codes[:, columns].bitcast(FP8X4),
+                scales=x_scales[:, columns],
+                in_=x_grouped[:],
+            )
+
+        regrouped = []
+
+        def quantise_and_multiply(job):
+            grouped, codes, scales, multiply, index = job
+            if codes is None:
+                codes = codes_pool.tile([P, CHUNK], U32, align_bytes=64, name="codes")[:]
+                scales = codes_pool.tile([P, CHUNK], U8, align_bytes=64, name="scales")[:]
+            nc.vector.quantize_mx(
+                out=codes.bitcast(FP8X4),
+                scales=scales,
+                in_=grouped[:].rearrange("p w t -> p (w t)"),
+            )
+            if multiply is not None:
+                multiply(index, codes, scales)
+
+        def step(pieces, codes, scales, multiply, index):
+            grouped = grouped_pool.tile([P, CHUNK, PACK], BF16, align_bytes=64, name="grouped")
+            for raw_piece, first in pieces:
+                nc.any.tensor_copy(
+                    out=grouped[:, first : first + PIECE, :].rearrange("p (c i) t -> p c t i", i=RUN),
+                    in_=raw_piece.rearrange("p t (c i) -> p c t i", i=RUN),
+                )
+            regrouped.append((grouped, codes, scales, multiply, index))
+            if len(regrouped) > LAG:
+                quantise_and_multiply(regrouped[-1 - LAG])
+
+        def column_pieces(rows):
+            return [(rows[:, :, first : first + PIECE], first) for first in range(0, CHUNK, PIECE)]
+
+        h_acc = [bank(4 + m, "h_acc%d" % m) for m in range(TOKEN_TILES)]
+
+        def project(j, codes, scales):
+            for b in range(BLOCKS):
+                c = BLOCKS * j + b
+                columns = slice(BANK * b, BANK * (b + 1))
+                for m in range(TOKEN_TILES):
+                    tokens = slice(TOKENS * c + P * m, TOKENS * c + P * (m + 1))
+                    nc.tensor.matmul_mx(
+                        out=h_acc[m],
+                        lhsT=x_codes[:, tokens].bitcast(FP8X4),
+                        lhsT_scale=x_scales[:, tokens],
+                        rhs=codes[:, columns].bitcast(FP8X4),
+                        rhs_scale=scales[:, columns],
+                        start=(c == 0),
+                        stop=(c == PASSES - 1),
+                    )
+
+        X_PERIOD = X_PASSES // BLOCKS
+        for j in range(PASSES // BLOCKS):
+            raw = raw_pool.tile([P, CHUNK * PACK], BF16, name="raw")
+            passes = raw[:].rearrange("p (c t w) -> p c t w", c=BLOCKS, t=PACK)
+            for b in range(BLOCKS):
+                c = BLOCKS * j + b
+                nc.sync.dma_start(
+                    out=passes[:, b],
+                    in_=tail_proj_0[K_PASS * c : K_PASS * (c + 1), :].rearrange(
+                        "(p t) w -> p t w", t=PACK
+                    ),
+                )
+            pieces = [
+                (passes[:, b, :, first : first + PIECE], BANK * b + first)
+                for b in range(BLOCKS)
+                for first in range(0, BANK, PIECE)
+            ]
+            step(pieces, None, None, project, j)
+            if j % X_PERIOD == 0:
+                x_grouped = transpose_x(j // X_PERIOD)
+            if j % X_PERIOD == 1:
+                quantise_x(j // X_PERIOD, x_grouped)
+
+        tail_codes = keep.tile([P, TAIL], U32, align_bytes=64, name="tail_codes")
+        tail_scales = keep.tile([P, TAIL], U8, align_bytes=64, name="tail_scales")
+        tail_rows = tail_w_0.rearrange("(p t) n -> p t n", t=PACK)
+        for i in range(TAIL // CHUNK):
+            columns = slice(CHUNK * i, CHUNK * (i + 1))
+            raw = raw_pool.tile([P, CHUNK * PACK], BF16, name="raw")
+            rows = raw[:].rearrange("p (t w) -> p t w", t=PACK)
+            nc.sync.dma_start(out=rows, in_=tail_rows[:, :, columns])
+            step(column_pieces(rows), tail_codes[:, columns], tail_scales[:, columns], None, i)
+
+        h_rounded = [keep.tile([P, PROJ], BF16, name="h_rounded%d" % m) for m in range(TOKEN_TILES)]
+        h_grouped = keep.tile([P, TOKENS, PACK], BF16, align_bytes=64, name="h_grouped")
+        h_codes = keep.tile([P, TOKENS], U32, align_bytes=64, name="h_codes")
+        h_scales = keep.tile([P, TOKENS], U8, align_bytes=64, name="h_scales")
+        TAIL_BANKS = TAIL // BANK
+        tail_logits = {}
+        tail_exp = [keep.tile([P, TAIL], F32, name="tail_exp%d" % m) for m in range(TOKEN_TILES)]
+        tail_bank_max = [
+            keep.tile([P, TAIL_BANKS], F32, name="tail_bank_max%d" % m) for m in range(TOKEN_TILES)
+        ]
+        tail_neg_max = [keep.tile([P, 1], F32, name="tail_neg_max%d" % m) for m in range(TOKEN_TILES)]
+        tail_bank_sum = [
+            keep.tile([P, TAIL_BANKS], F32, name="tail_bank_sum%d" % m) for m in range(TOKEN_TILES)
+        ]
+        tail_sum = [keep.tile([P, 1], F32, name="tail_sum%d" % m) for m in range(TOKEN_TILES)]
+        tail_inverse = [keep.tile([P, 1], F32, name="tail_inverse%d" % m) for m in range(TOKEN_TILES)]
+
+        def round_h():
+            for m in range(TOKEN_TILES):
+                copy = nc.vector.tensor_copy if m == 0 else nc.scalar.copy
+                copy(out=h_rounded[m][:], in_=h_acc[m])
+
+        def regroup_h():
+            ht = bank(6, "ht").rearrange("p (u r) -> p u r", u=2)
+            for u in range(2):
+                for m in range(TOKEN_TILES):
+                    words = h_rounded[m][:].bitcast(F32).rearrange("r (p u) -> r u p", u=2)
+                    nc.tensor.transpose(ht[:, u, P * m : P * (m + 1)], words[:, u, :], identity[:])
+            nc.vector.tensor_copy(
+                out=h_grouped[:].rearrange("p r t -> p (r t)").bitcast(F32).rearrange(
+                    "p (r u) -> p r u", u=2
+                ),
+                in_=ht.rearrange("p u r -> p r u"),
+            )
+
+        def quantise_h():
+            nc.vector.quantize_mx(
+                out=h_codes[:].bitcast(FP8X4),
+                scales=h_scales[:],
+                in_=h_grouped[:].rearrange("p r t -> p (r t)"),
+            )
+
+        def multiply_tail(m):
+            tokens = slice(P * m, P * (m + 1))
+            for n in range(TAIL_BANKS):
+                columns = slice(BANK * n, BANK * (n + 1))
+                tail_logits[(m, n)] = bank(4 + n, "tail_logits")
+                nc.tensor.matmul_mx(
+                    out=tail_logits[(m, n)],
+                    lhsT=h_codes[:, tokens].bitcast(FP8X4),
+                    lhsT_scale=h_scales[:, tokens],
+                    rhs=tail_codes[:, columns].bitcast(FP8X4),
+                    rhs_scale=tail_scales[:, columns],
+                    start=True,
+                    stop=True,
+                )
+
+        def max_tail(m):
+            for n in range(TAIL_BANKS):
+                nc.vector.reduce_max(
+                    out=tail_bank_max[m][:, n : n + 1], in_=tail_logits[(m, n)], axis=ALONG_ROW
+                )
+            nc.vector.tensor_reduce(
+                out=tail_neg_max[m][:], in_=tail_bank_max[m][:], axis=ALONG_ROW, op=MAX, negate=True
+            )
+
+        def exp_tail(m):
+            for n in range(TAIL_BANKS):
+                nc.scalar.activation(
+                    out=tail_exp[m][:, BANK * n : BANK * (n + 1)],
+                    in_=tail_logits[(m, n)],
+                    func=EXP,
+                    bias=tail_neg_max[m][:],
+                    accum_out=tail_bank_sum[m][:, n : n + 1],
+                )
+
+        def invert_tail_sum(m):
+            nc.vector.reduce_sum(out=tail_sum[m][:], in_=tail_bank_sum[m][:], axis=ALONG_ROW)
+            nc.vector.reciprocal(out=tail_inverse[m][:], in_=tail_sum[m][:])
+
+        tail_stages = [round_h, regroup_h, quantise_h]
+        for m in range(TOKEN_TILES):
+            tail_stages.extend([lambda m=m: multiply_tail(m), lambda m=m: max_tail(m)])
+            if m < TOKEN_TILES - 1:
+                tail_stages.extend([lambda m=m: exp_tail(m), lambda m=m: invert_tail_sum(m)])
+
+        HEAD_BANKS = HEAD // BANK
+        head_acc = [
+            [bank(HEAD_BANKS * m + n, "head_acc%d%d" % (m, n)) for n in range(HEAD_BANKS)]
+            for m in range(TOKEN_TILES)
+        ]
+
+        def multiply_head(c, codes, scales):
+            for m in range(TOKEN_TILES):
+                tokens = slice(TOKENS * c + P * m, TOKENS * c + P * (m + 1))
+                for n in range(HEAD_BANKS):
+                    columns = slice(BANK * n, BANK * (n + 1))
+                    nc.tensor.matmul_mx(
+                        out=head_acc[m][n],
+                        lhsT=x_codes[:, tokens].bitcast(FP8X4),
+                        lhsT_scale=x_scales[:, tokens],
+                        rhs=codes[:, columns].bitcast(FP8X4),
+                        rhs_scale=scales[:, columns],
+                        start=(c == 0),
+                        stop=(c == PASSES - 1),
+                    )
+
+        for c in range(PASSES):
+            raw = raw_pool.tile([P, CHUNK * PACK], BF16, name="raw")
+            rows = raw[:].rearrange("p (t w) -> p t w", t=PACK)
+            nc.sync.dma_start(
+                out=rows,
+                in_=head_weight[K_PASS * c : K_PASS * (c + 1), :].rearrange(
+                    "(p t) w -> p t w", t=PACK
+                ),
+            )
+            step(column_pieces(rows), None, None, multiply_head, c)
+            if c < len(tail_stages):
+                tail_stages[c]()
+        for job in regrouped[-LAG:]:
+            quantise_and_multiply(job)
+        exp_tail(TOKEN_TILES - 1)
+        invert_tail_sum(TOKEN_TILES - 1)
+
+        head_exp = [keep.tile([P, HEAD], F32, name="head_exp%d" % m) for m in range(TOKEN_TILES)]
+        head_bank_max = [
+            keep.tile([P, HEAD_BANKS], F32, name="head_bank_max%d" % m) for m in range(TOKEN_TILES)
+        ]
+        head_neg_max = [keep.tile([P, 1], F32, name="head_neg_max%d" % m) for m in range(TOKEN_TILES)]
+        head_bank_sum = [
+            keep.tile([P, HEAD_BANKS], F32, name="head_bank_sum%d" % m) for m in range(TOKEN_TILES)
+        ]
+        head_sum = [keep.tile([P, 1], F32, name="head_sum%d" % m) for m in range(TOKEN_TILES)]
+        head_inverse = [keep.tile([P, 1], F32, name="head_inverse%d" % m) for m in range(TOKEN_TILES)]
+        tail_factor = [keep.tile([P, 1], F32, name="tail_factor%d" % m) for m in range(TOKEN_TILES)]
+
+        for m in range(TOKEN_TILES):
+            for n in range(HEAD_BANKS):
+                nc.vector.reduce_max(
+                    out=head_bank_max[m][:, n : n + 1], in_=head_acc[m][n], axis=ALONG_ROW
+                )
+            nc.vector.tensor_reduce(
+                out=head_neg_max[m][:], in_=head_bank_max[m][:], axis=ALONG_ROW, op=MAX, negate=True
+            )
+        for m in range(TOKEN_TILES):
+            for n in range(HEAD_BANKS):
+                nc.scalar.activation(
+                    out=head_exp[m][:, BANK * n : BANK * (n + 1)],
+                    in_=head_acc[m][n],
+                    func=EXP,
+                    bias=head_neg_max[m][:],
+                    accum_out=head_bank_sum[m][:, n : n + 1],
+                )
+        for m in range(TOKEN_TILES):
+            nc.vector.reduce_sum(out=head_sum[m][:], in_=head_bank_sum[m][:], axis=ALONG_ROW)
+            nc.vector.reciprocal(out=head_inverse[m][:], in_=head_sum[m][:])
+            nc.vector.tensor_scalar(
+                out=tail_factor[m][:],
+                in0=head_exp[m][:, HEAD_TOKENS : HEAD_TOKENS + 1],
+                scalar1=head_inverse[m][:],
+                scalar2=tail_inverse[m][:],
+                op0=MULT,
+                op1=MULT,
+            )
+            nc.vector.tensor_scalar(
+                out=cluster1[:, m : m + 1],
+                in0=head_exp[m][:, HEAD_TOKENS + 1 : HEAD_TOKENS + 2],
+                scalar1=head_inverse[m][:],
+                scalar2=None,
+                op0=MULT,
+            )
+            for first in range(0, TAIL, STORE_COLUMNS):
+                columns = slice(first, first + STORE_COLUMNS)
+                nc.vector.tensor_scalar(
+                    out=tail_exp[m][:, columns],
+                    in0=tail_exp[m][:, columns],
+                    scalar1=tail_factor[m][:],
+                    scalar2=None,
+                    op0=MULT,
+                )
+                nc.sync.dma_start(
+                    out=out_0[m, :, HEAD_TOKENS + first : HEAD_TOKENS + first + STORE_COLUMNS],
+                    in_=tail_exp[m][:, columns],
+                )
+            nc.scalar.activation(
+                out=head_exp[m][:, 0:HEAD_TOKENS],
+                in_=head_exp[m][:, 0:HEAD_TOKENS],
+                func=COPY,
+                scale=head_inverse[m][:],
+            )
+            nc.sync.dma_start(out=out_0[m, :, 0:HEAD_TOKENS], in_=head_exp[m][:, 0:HEAD_TOKENS])
+
+        cluster1_rows = bank(4, "cluster1_rows")
+        nc.tensor.transpose(cluster1_rows[:, 0:P], cluster1[:], identity[:])
+        cluster1_out = keep.tile([P, P], F32, name="cluster1_out")
+        nc.scalar.copy(out=cluster1_out[:], in_=cluster1_rows[:, 0:P])
+        nc.sync.dma_start(
+            out=out_1.rearrange("n t o -> n (t o)"), in_=cluster1_out[0:TOKEN_TILES, :]
+        )

@@ -12,6 +12,7 @@ EXP = mybir.ActivationFunctionType.Exp
 COPY = mybir.ActivationFunctionType.Copy
 MULT = mybir.AluOpType.mult
 MAX = mybir.AluOpType.max
+MIN = mybir.AluOpType.min
 ALONG_ROW = mybir.AxisListType.X
 
 P = 128
@@ -31,10 +32,12 @@ TAIL = 2048
 BLOCKS = 2
 CHUNK = BLOCKS * BANK
 X_PASSES = 4
-STORE_COLUMNS = 1024
 LAG = 2
 PIECE = 256
+VECTOR, SCALAR, TENSOR = 0, 1, 2
 RUN = 4
+
+TAIL_BANK_ORDER = (0, 1, 2, 3, 7, 4, 5, 6)
 
 FLOPS = 2 * TOKENS * D * (HEAD + PROJ) + 2 * TOKENS * PROJ * TAIL
 
@@ -47,7 +50,8 @@ def tile_adaptiveinputsoftmax_pa_k_kernel(
         keep = ctx.enter_context(tc.tile_pool(name="keep", bufs=1))
         x_pool = ctx.enter_context(tc.tile_pool(name="x_pool", bufs=4))
         x_grouped_pool = ctx.enter_context(tc.tile_pool(name="x_grouped_pool", bufs=2))
-        raw_pool = ctx.enter_context(tc.tile_pool(name="raw_pool", bufs=8))
+        wide_pool = ctx.enter_context(tc.tile_pool(name="wide_pool", bufs=6))
+        narrow_pool = ctx.enter_context(tc.tile_pool(name="narrow_pool", bufs=12))
         grouped_pool = ctx.enter_context(tc.tile_pool(name="grouped_pool", bufs=LAG + 2))
         codes_pool = ctx.enter_context(tc.tile_pool(name="codes_pool", bufs=3))
         psum = ctx.enter_context(tc.psum_pool(name="psum", bufs=1))
@@ -57,6 +61,8 @@ def tile_adaptiveinputsoftmax_pa_k_kernel(
 
         identity = keep.tile([P, P], F32, name="identity")
         make_identity(nc, identity[:])
+        identity_bf16 = keep.tile([P, P], BF16, name="identity_bf16")
+        make_identity(nc, identity_bf16[:])
         zero = keep.tile([P, 1], F32, name="zero")
         one = keep.tile([P, 1], F32, name="one")
         nc.vector.memset(zero[:], 0.0)
@@ -83,7 +89,7 @@ def tile_adaptiveinputsoftmax_pa_k_kernel(
                 "p (g r u) -> p g r u", g=X_PASSES, u=2
             )
             for g in range(X_PASSES):
-                xt = bank(g, "xt").rearrange("p (u r) -> p u r", u=2)
+                xt = bank(4 + (X_PASSES * a + g) % 3, "xt").rearrange("p (u r) -> p u r", u=2)
                 for u in range(2):
                     for m in range(TOKEN_TILES):
                         nc.tensor.transpose(
@@ -103,168 +109,73 @@ def tile_adaptiveinputsoftmax_pa_k_kernel(
         regrouped = []
 
         def quantise_and_multiply(job):
-            grouped, codes, scales, multiply, index = job
-            if codes is None:
-                codes = codes_pool.tile([P, CHUNK], U32, align_bytes=64, name="codes")[:]
-                scales = codes_pool.tile([P, CHUNK], U8, align_bytes=64, name="scales")[:]
+            grouped, width, multiply, index = job
+            codes = codes_pool.tile([P, CHUNK], U32, align_bytes=64, name="codes")[:, 0:width]
+            scales = codes_pool.tile([P, CHUNK], U8, align_bytes=64, name="scales")[:, 0:width]
             nc.vector.quantize_mx(
                 out=codes.bitcast(FP8X4),
                 scales=scales,
-                in_=grouped[:].rearrange("p w t -> p (w t)"),
+                in_=grouped[:, 0:width, :].rearrange("p w t -> p (w t)"),
             )
-            if multiply is not None:
-                multiply(index, codes, scales)
+            multiply(index, codes, scales)
 
-        def step(pieces, codes, scales, multiply, index):
-            grouped = grouped_pool.tile([P, CHUNK, PACK], BF16, align_bytes=64, name="grouped")
-            for raw_piece, first in pieces:
-                nc.any.tensor_copy(
-                    out=grouped[:, first : first + PIECE, :].rearrange("p (c i) t -> p c t i", i=RUN),
-                    in_=raw_piece.rearrange("p t (c i) -> p c t i", i=RUN),
+        def interleaved(view):
+            return view.rearrange("p (c i) t -> p c t i", i=RUN)
+
+        def regroup(engine, target, source):
+            if engine == TENSOR:
+                bank7 = psum.tile([P, PIECE, PACK], BF16, tag="bank7", name="bank7")
+                for first in range(0, PIECE, P):
+                    columns = slice(first, first + P)
+                    nc.tensor.matmul(
+                        out=interleaved(bank7[:, columns, :]),
+                        lhsT=identity_bf16[:],
+                        rhs=source[:, :, columns].rearrange("p t (c i) -> p c t i", i=RUN),
+                        start=True,
+                        stop=True,
+                    )
+                nc.scalar.copy(out=target, in_=bank7[:])
+            else:
+                copy = nc.vector.tensor_copy if engine == VECTOR else nc.scalar.copy
+                copy(
+                    out=interleaved(target), in_=source.rearrange("p t (c i) -> p c t i", i=RUN)
                 )
-            regrouped.append((grouped, codes, scales, multiply, index))
+
+        def step(rows, shares, multiply, index):
+            grouped = grouped_pool.tile([P, CHUNK, PACK], BF16, align_bytes=64, name="grouped")
+            width = 0
+            for view, parts in zip(rows, shares):
+                first = 0
+                for engine, columns in parts:
+                    regroup(
+                        engine,
+                        grouped[:, width : width + columns, :],
+                        view[:, :, first : first + columns],
+                    )
+                    first += columns
+                    width += columns
+            regrouped.append((grouped, width, multiply, index))
             if len(regrouped) > LAG:
                 quantise_and_multiply(regrouped[-1 - LAG])
 
-        def column_pieces(rows):
-            return [(rows[:, :, first : first + PIECE], first) for first in range(0, CHUNK, PIECE)]
+        def load(source):
+            width = source.shape[1]
+            pool = wide_pool if width == HEAD else narrow_pool
+            raw = pool.tile([P, PACK, width], BF16, name="raw")
+            nc.sync.dma_start(out=raw[:], in_=source.rearrange("(p t) w -> p t w", t=PACK))
+            return raw[:]
 
-        h_acc = [bank(4 + m, "h_acc%d" % m) for m in range(TOKEN_TILES)]
-
-        def project(j, codes, scales):
-            for b in range(BLOCKS):
-                c = BLOCKS * j + b
-                columns = slice(BANK * b, BANK * (b + 1))
-                for m in range(TOKEN_TILES):
-                    tokens = slice(TOKENS * c + P * m, TOKENS * c + P * (m + 1))
-                    nc.tensor.matmul_mx(
-                        out=h_acc[m],
-                        lhsT=x_codes[:, tokens].bitcast(FP8X4),
-                        lhsT_scale=x_scales[:, tokens],
-                        rhs=codes[:, columns].bitcast(FP8X4),
-                        rhs_scale=scales[:, columns],
-                        start=(c == 0),
-                        stop=(c == PASSES - 1),
-                    )
-
-        X_PERIOD = X_PASSES // BLOCKS
-        for j in range(PASSES // BLOCKS):
-            raw = raw_pool.tile([P, CHUNK * PACK], BF16, name="raw")
-            passes = raw[:].rearrange("p (c t w) -> p c t w", c=BLOCKS, t=PACK)
-            for b in range(BLOCKS):
-                c = BLOCKS * j + b
-                nc.sync.dma_start(
-                    out=passes[:, b],
-                    in_=tail_proj_0[K_PASS * c : K_PASS * (c + 1), :].rearrange(
-                        "(p t) w -> p t w", t=PACK
-                    ),
-                )
-            pieces = [
-                (passes[:, b, :, first : first + PIECE], BANK * b + first)
-                for b in range(BLOCKS)
-                for first in range(0, BANK, PIECE)
-            ]
-            step(pieces, None, None, project, j)
-            if j % X_PERIOD == 0:
-                x_grouped = transpose_x(j // X_PERIOD)
-            if j % X_PERIOD == 1:
-                quantise_x(j // X_PERIOD, x_grouped)
-
-        tail_codes = keep.tile([P, TAIL], U32, align_bytes=64, name="tail_codes")
-        tail_scales = keep.tile([P, TAIL], U8, align_bytes=64, name="tail_scales")
-        tail_rows = tail_w_0.rearrange("(p t) n -> p t n", t=PACK)
-        for i in range(TAIL // CHUNK):
-            columns = slice(CHUNK * i, CHUNK * (i + 1))
-            raw = raw_pool.tile([P, CHUNK * PACK], BF16, name="raw")
-            rows = raw[:].rearrange("p (t w) -> p t w", t=PACK)
-            nc.sync.dma_start(out=rows, in_=tail_rows[:, :, columns])
-            step(column_pieces(rows), tail_codes[:, columns], tail_scales[:, columns], None, i)
-
-        h_rounded = [keep.tile([P, PROJ], BF16, name="h_rounded%d" % m) for m in range(TOKEN_TILES)]
-        h_grouped = keep.tile([P, TOKENS, PACK], BF16, align_bytes=64, name="h_grouped")
-        h_codes = keep.tile([P, TOKENS], U32, align_bytes=64, name="h_codes")
-        h_scales = keep.tile([P, TOKENS], U8, align_bytes=64, name="h_scales")
-        TAIL_BANKS = TAIL // BANK
-        tail_logits = {}
-        tail_exp = [keep.tile([P, TAIL], F32, name="tail_exp%d" % m) for m in range(TOKEN_TILES)]
-        tail_bank_max = [
-            keep.tile([P, TAIL_BANKS], F32, name="tail_bank_max%d" % m) for m in range(TOKEN_TILES)
-        ]
-        tail_neg_max = [keep.tile([P, 1], F32, name="tail_neg_max%d" % m) for m in range(TOKEN_TILES)]
-        tail_bank_sum = [
-            keep.tile([P, TAIL_BANKS], F32, name="tail_bank_sum%d" % m) for m in range(TOKEN_TILES)
-        ]
-        tail_sum = [keep.tile([P, 1], F32, name="tail_sum%d" % m) for m in range(TOKEN_TILES)]
-        tail_inverse = [keep.tile([P, 1], F32, name="tail_inverse%d" % m) for m in range(TOKEN_TILES)]
-
-        def round_h():
-            for m in range(TOKEN_TILES):
-                copy = nc.vector.tensor_copy if m == 0 else nc.scalar.copy
-                copy(out=h_rounded[m][:], in_=h_acc[m])
-
-        def regroup_h():
-            ht = bank(6, "ht").rearrange("p (u r) -> p u r", u=2)
-            for u in range(2):
-                for m in range(TOKEN_TILES):
-                    words = h_rounded[m][:].bitcast(F32).rearrange("r (p u) -> r u p", u=2)
-                    nc.tensor.transpose(ht[:, u, P * m : P * (m + 1)], words[:, u, :], identity[:])
-            nc.vector.tensor_copy(
-                out=h_grouped[:].rearrange("p r t -> p (r t)").bitcast(F32).rearrange(
-                    "p (r u) -> p r u", u=2
-                ),
-                in_=ht.rearrange("p u r -> p r u"),
+        def multiply_pass(out, c, m, codes, scales, columns, start, stop):
+            tokens = slice(TOKENS * c + P * m, TOKENS * c + P * (m + 1))
+            nc.tensor.matmul_mx(
+                out=out,
+                lhsT=x_codes[:, tokens].bitcast(FP8X4),
+                lhsT_scale=x_scales[:, tokens],
+                rhs=codes[:, columns].bitcast(FP8X4),
+                rhs_scale=scales[:, columns],
+                start=start,
+                stop=stop,
             )
-
-        def quantise_h():
-            nc.vector.quantize_mx(
-                out=h_codes[:].bitcast(FP8X4),
-                scales=h_scales[:],
-                in_=h_grouped[:].rearrange("p r t -> p (r t)"),
-            )
-
-        def multiply_tail(m):
-            tokens = slice(P * m, P * (m + 1))
-            for n in range(TAIL_BANKS):
-                columns = slice(BANK * n, BANK * (n + 1))
-                tail_logits[(m, n)] = bank(4 + n, "tail_logits")
-                nc.tensor.matmul_mx(
-                    out=tail_logits[(m, n)],
-                    lhsT=h_codes[:, tokens].bitcast(FP8X4),
-                    lhsT_scale=h_scales[:, tokens],
-                    rhs=tail_codes[:, columns].bitcast(FP8X4),
-                    rhs_scale=tail_scales[:, columns],
-                    start=True,
-                    stop=True,
-                )
-
-        def max_tail(m):
-            for n in range(TAIL_BANKS):
-                nc.vector.reduce_max(
-                    out=tail_bank_max[m][:, n : n + 1], in_=tail_logits[(m, n)], axis=ALONG_ROW
-                )
-            nc.vector.tensor_reduce(
-                out=tail_neg_max[m][:], in_=tail_bank_max[m][:], axis=ALONG_ROW, op=MAX, negate=True
-            )
-
-        def exp_tail(m):
-            for n in range(TAIL_BANKS):
-                nc.scalar.activation(
-                    out=tail_exp[m][:, BANK * n : BANK * (n + 1)],
-                    in_=tail_logits[(m, n)],
-                    func=EXP,
-                    bias=tail_neg_max[m][:],
-                    accum_out=tail_bank_sum[m][:, n : n + 1],
-                )
-
-        def invert_tail_sum(m):
-            nc.vector.reduce_sum(out=tail_sum[m][:], in_=tail_bank_sum[m][:], axis=ALONG_ROW)
-            nc.vector.reciprocal(out=tail_inverse[m][:], in_=tail_sum[m][:])
-
-        tail_stages = [round_h, regroup_h, quantise_h]
-        for m in range(TOKEN_TILES):
-            tail_stages.extend([lambda m=m: multiply_tail(m), lambda m=m: max_tail(m)])
-            if m < TOKEN_TILES - 1:
-                tail_stages.extend([lambda m=m: exp_tail(m), lambda m=m: invert_tail_sum(m)])
 
         HEAD_BANKS = HEAD // BANK
         head_acc = [
@@ -274,35 +185,25 @@ def tile_adaptiveinputsoftmax_pa_k_kernel(
 
         def multiply_head(c, codes, scales):
             for m in range(TOKEN_TILES):
-                tokens = slice(TOKENS * c + P * m, TOKENS * c + P * (m + 1))
                 for n in range(HEAD_BANKS):
                     columns = slice(BANK * n, BANK * (n + 1))
-                    nc.tensor.matmul_mx(
-                        out=head_acc[m][n],
-                        lhsT=x_codes[:, tokens].bitcast(FP8X4),
-                        lhsT_scale=x_scales[:, tokens],
-                        rhs=codes[:, columns].bitcast(FP8X4),
-                        rhs_scale=scales[:, columns],
-                        start=(c == 0),
-                        stop=(c == PASSES - 1),
+                    multiply_pass(
+                        head_acc[m][n], c, m, codes, scales, columns, c == 0, c == PASSES - 1
                     )
 
         for c in range(PASSES):
-            raw = raw_pool.tile([P, CHUNK * PACK], BF16, name="raw")
-            rows = raw[:].rearrange("p (t w) -> p t w", t=PACK)
-            nc.sync.dma_start(
-                out=rows,
-                in_=head_weight[K_PASS * c : K_PASS * (c + 1), :].rearrange(
-                    "(p t) w -> p t w", t=PACK
-                ),
-            )
-            step(column_pieces(rows), None, None, multiply_head, c)
-            if c < len(tail_stages):
-                tail_stages[c]()
-        for job in regrouped[-LAG:]:
-            quantise_and_multiply(job)
-        exp_tail(TOKEN_TILES - 1)
-        invert_tail_sum(TOKEN_TILES - 1)
+            weight = head_weight[K_PASS * c : K_PASS * (c + 1), :]
+            if c == 0:
+                rows = [load(weight[:, 0:BANK]), load(weight[:, BANK:HEAD])]
+                shares = [[(VECTOR, 256), (SCALAR, 256)], [(VECTOR, 256), (TENSOR, 256)]]
+            else:
+                rows = [load(weight)]
+                shares = [[(SCALAR, 256), (VECTOR, 512), (TENSOR, 256)]]
+            step(rows, shares, multiply_head, c)
+            if c % X_PASSES == 0:
+                x_grouped = transpose_x(c // X_PASSES)
+            if c % X_PASSES == 1:
+                quantise_x(c // X_PASSES, x_grouped)
 
         head_exp = [keep.tile([P, HEAD], F32, name="head_exp%d" % m) for m in range(TOKEN_TILES)]
         head_bank_max = [
@@ -314,9 +215,9 @@ def tile_adaptiveinputsoftmax_pa_k_kernel(
         ]
         head_sum = [keep.tile([P, 1], F32, name="head_sum%d" % m) for m in range(TOKEN_TILES)]
         head_inverse = [keep.tile([P, 1], F32, name="head_inverse%d" % m) for m in range(TOKEN_TILES)]
-        tail_factor = [keep.tile([P, 1], F32, name="tail_factor%d" % m) for m in range(TOKEN_TILES)]
+        cluster0 = [keep.tile([P, 1], F32, name="cluster0_%d" % m) for m in range(TOKEN_TILES)]
 
-        for m in range(TOKEN_TILES):
+        def max_head(m):
             for n in range(HEAD_BANKS):
                 nc.vector.reduce_max(
                     out=head_bank_max[m][:, n : n + 1], in_=head_acc[m][n], axis=ALONG_ROW
@@ -324,7 +225,8 @@ def tile_adaptiveinputsoftmax_pa_k_kernel(
             nc.vector.tensor_reduce(
                 out=head_neg_max[m][:], in_=head_bank_max[m][:], axis=ALONG_ROW, op=MAX, negate=True
             )
-        for m in range(TOKEN_TILES):
+
+        def exp_head(m):
             for n in range(HEAD_BANKS):
                 nc.scalar.activation(
                     out=head_exp[m][:, BANK * n : BANK * (n + 1)],
@@ -333,49 +235,189 @@ def tile_adaptiveinputsoftmax_pa_k_kernel(
                     bias=head_neg_max[m][:],
                     accum_out=head_bank_sum[m][:, n : n + 1],
                 )
-        for m in range(TOKEN_TILES):
+
+        def finish_head(m):
             nc.vector.reduce_sum(out=head_sum[m][:], in_=head_bank_sum[m][:], axis=ALONG_ROW)
             nc.vector.reciprocal(out=head_inverse[m][:], in_=head_sum[m][:])
+            for column, target in ((0, cluster0[m][:]), (1, cluster1[:, m : m + 1])):
+                nc.vector.tensor_scalar(
+                    out=target,
+                    in0=head_exp[m][:, HEAD_TOKENS + column : HEAD_TOKENS + column + 1],
+                    scalar1=head_inverse[m][:],
+                    scalar2=None,
+                    op0=MULT,
+                )
             nc.vector.tensor_scalar(
-                out=tail_factor[m][:],
-                in0=head_exp[m][:, HEAD_TOKENS : HEAD_TOKENS + 1],
-                scalar1=head_inverse[m][:],
-                scalar2=tail_inverse[m][:],
-                op0=MULT,
-                op1=MULT,
-            )
-            nc.vector.tensor_scalar(
-                out=cluster1[:, m : m + 1],
-                in0=head_exp[m][:, HEAD_TOKENS + 1 : HEAD_TOKENS + 2],
+                out=head_exp[m][:, 0:HEAD_TOKENS],
+                in0=head_exp[m][:, 0:HEAD_TOKENS],
                 scalar1=head_inverse[m][:],
                 scalar2=None,
                 op0=MULT,
             )
-            for first in range(0, TAIL, STORE_COLUMNS):
-                columns = slice(first, first + STORE_COLUMNS)
-                nc.vector.tensor_scalar(
-                    out=tail_exp[m][:, columns],
-                    in0=tail_exp[m][:, columns],
-                    scalar1=tail_factor[m][:],
-                    scalar2=None,
-                    op0=MULT,
-                )
-                nc.sync.dma_start(
-                    out=out_0[m, :, HEAD_TOKENS + first : HEAD_TOKENS + first + STORE_COLUMNS],
-                    in_=tail_exp[m][:, columns],
-                )
-            nc.scalar.activation(
-                out=head_exp[m][:, 0:HEAD_TOKENS],
-                in_=head_exp[m][:, 0:HEAD_TOKENS],
-                func=COPY,
-                scale=head_inverse[m][:],
-            )
             nc.sync.dma_start(out=out_0[m, :, 0:HEAD_TOKENS], in_=head_exp[m][:, 0:HEAD_TOKENS])
 
-        cluster1_rows = bank(4, "cluster1_rows")
-        nc.tensor.transpose(cluster1_rows[:, 0:P], cluster1[:], identity[:])
-        cluster1_out = keep.tile([P, P], F32, name="cluster1_out")
-        nc.scalar.copy(out=cluster1_out[:], in_=cluster1_rows[:, 0:P])
-        nc.sync.dma_start(
-            out=out_1.rearrange("n t o -> n (t o)"), in_=cluster1_out[0:TOKEN_TILES, :]
-        )
+        def store_cluster1():
+            cluster1_rows = bank(7, "cluster1_rows")
+            nc.tensor.transpose(cluster1_rows[:, 0:P], cluster1[:], identity[:])
+            cluster1_out = keep.tile([P, P], F32, name="cluster1_out")
+            nc.scalar.copy(out=cluster1_out[:], in_=cluster1_rows[:, 0:P])
+            nc.sync.dma_start(
+                out=out_1.rearrange("n t o -> n (t o)"), in_=cluster1_out[0:TOKEN_TILES, :]
+            )
+
+        head_stages = [stage for m in range(TOKEN_TILES) for stage in (
+            lambda m=m: max_head(m), lambda m=m: exp_head(m), lambda m=m: finish_head(m)
+        )]
+        head_stages.append(store_cluster1)
+
+        h_acc = [bank(4 + m, "h_acc%d" % m) for m in range(TOKEN_TILES)]
+
+        def project(j, codes, scales):
+            for b in range(BLOCKS):
+                c = BLOCKS * j + b
+                columns = slice(BANK * b, BANK * (b + 1))
+                for m in range(TOKEN_TILES):
+                    multiply_pass(h_acc[m], c, m, codes, scales, columns, c == 0, c == PASSES - 1)
+
+        for j in range(PASSES // BLOCKS):
+            rows = [
+                load(tail_proj_0[K_PASS * c : K_PASS * (c + 1), :])
+                for c in range(BLOCKS * j, BLOCKS * (j + 1))
+            ]
+            step(rows, [[(VECTOR, 256), (SCALAR, 256)]] * BLOCKS, project, j)
+            if LAG - 1 <= j < LAG - 1 + len(head_stages):
+                head_stages[j - LAG + 1]()
+
+        h_rounded = [keep.tile([P, PROJ], BF16, name="h_rounded%d" % m) for m in range(TOKEN_TILES)]
+        h_grouped = keep.tile([P, TOKENS, PACK], BF16, align_bytes=64, name="h_grouped")
+        h_codes = keep.tile([P, TOKENS], U32, align_bytes=64, name="h_codes")
+        h_scales = keep.tile([P, TOKENS], U8, align_bytes=64, name="h_scales")
+
+        def quantise_h():
+            for m in range(TOKEN_TILES):
+                copy = nc.vector.tensor_copy if m == 0 else nc.scalar.copy
+                copy(out=h_rounded[m][:], in_=h_acc[m])
+            ht = bank(6, "ht").rearrange("p (u r) -> p u r", u=2)
+            for u in range(2):
+                for m in range(TOKEN_TILES):
+                    words = h_rounded[m][:].bitcast(F32).rearrange("r (p u) -> r u p", u=2)
+                    nc.tensor.transpose(ht[:, u, P * m : P * (m + 1)], words[:, u, :], identity[:])
+            nc.vector.tensor_copy(
+                out=h_grouped[:].rearrange("p r t -> p (r t)").bitcast(F32).rearrange(
+                    "p (r u) -> p r u", u=2
+                ),
+                in_=ht.rearrange("p u r -> p r u"),
+            )
+            nc.vector.quantize_mx(
+                out=h_codes[:].bitcast(FP8X4),
+                scales=h_scales[:],
+                in_=h_grouped[:].rearrange("p r t -> p (r t)"),
+            )
+
+        TAIL_BANKS = TAIL // BANK
+        tail_exp = [keep.tile([P, TAIL], F32, name="tail_exp%d" % m) for m in range(TOKEN_TILES)]
+
+        def stats(name, width):
+            return [keep.tile([P, width], F32, name=name + str(m)) for m in range(TOKEN_TILES)]
+
+        bank_neg_max = stats("bank_neg_max", TAIL_BANKS)
+        bank_sum = stats("bank_sum", TAIL_BANKS)
+        tail_neg_max = stats("tail_neg_max", 1)
+        bank_factor = stats("bank_factor", TAIL_BANKS)
+        scaled_sum = stats("scaled_sum", TAIL_BANKS)
+        tail_sum = stats("tail_sum", 1)
+        tail_inverse = stats("tail_inverse", 1)
+        bank_scale = stats("bank_scale", TAIL_BANKS)
+
+        def multiply_tail(first_bank, codes, scales):
+            for i in range(codes.shape[1] // BANK):
+                n = first_bank + i
+                columns = slice(BANK * i, BANK * (i + 1))
+                logits = []
+                for m in range(TOKEN_TILES):
+                    tokens = slice(P * m, P * (m + 1))
+                    logits.append(bank(TAIL_BANK_ORDER[TOKEN_TILES * n + m], "tail_logits"))
+                    nc.tensor.matmul_mx(
+                        out=logits[m],
+                        lhsT=h_codes[:, tokens].bitcast(FP8X4),
+                        lhsT_scale=h_scales[:, tokens],
+                        rhs=codes[:, columns].bitcast(FP8X4),
+                        rhs_scale=scales[:, columns],
+                        start=True,
+                        stop=True,
+                    )
+                for m in range(TOKEN_TILES):
+                    nc.vector.tensor_reduce(
+                        out=bank_neg_max[m][:, n : n + 1],
+                        in_=logits[m],
+                        axis=ALONG_ROW,
+                        op=MAX,
+                        negate=True,
+                    )
+                    nc.scalar.activation(
+                        out=tail_exp[m][:, BANK * n : BANK * (n + 1)],
+                        in_=logits[m],
+                        func=EXP,
+                        bias=bank_neg_max[m][:, n : n + 1],
+                        accum_out=bank_sum[m][:, n : n + 1],
+                    )
+
+        def finish_tail(m):
+            nc.vector.tensor_reduce(
+                out=tail_neg_max[m][:], in_=bank_neg_max[m][:], axis=ALONG_ROW, op=MIN
+            )
+            nc.scalar.activation(
+                out=bank_factor[m][:],
+                in_=bank_neg_max[m][:],
+                func=EXP,
+                scale=-1.0,
+                bias=tail_neg_max[m][:],
+            )
+            nc.vector.tensor_tensor(
+                out=scaled_sum[m][:], in0=bank_factor[m][:], in1=bank_sum[m][:], op=MULT
+            )
+            nc.vector.reduce_sum(out=tail_sum[m][:], in_=scaled_sum[m][:], axis=ALONG_ROW)
+            nc.vector.reciprocal(out=tail_inverse[m][:], in_=tail_sum[m][:])
+            nc.vector.tensor_scalar(
+                out=bank_scale[m][:],
+                in0=bank_factor[m][:],
+                scalar1=tail_inverse[m][:],
+                scalar2=cluster0[m][:],
+                op0=MULT,
+                op1=MULT,
+            )
+
+        def store_tail(m):
+            for n in range(TAIL_BANKS):
+                columns = slice(BANK * n, BANK * (n + 1))
+                if n == TAIL_BANKS - 1:
+                    nc.scalar.activation(
+                        out=tail_exp[m][:, columns],
+                        in_=tail_exp[m][:, columns],
+                        func=COPY,
+                        scale=bank_scale[m][:, n : n + 1],
+                    )
+                else:
+                    nc.vector.tensor_scalar(
+                        out=tail_exp[m][:, columns],
+                        in0=tail_exp[m][:, columns],
+                        scalar1=bank_scale[m][:, n : n + 1],
+                        scalar2=None,
+                        op0=MULT,
+                    )
+                nc.sync.dma_start(
+                    out=out_0[m, :, HEAD_TOKENS + BANK * n : HEAD_TOKENS + BANK * (n + 1)],
+                    in_=tail_exp[m][:, columns],
+                )
+
+        for i in range(TAIL_BANKS):
+            columns = slice(BANK * i, BANK * (i + 1))
+            step([load(tail_w_0[:, columns])], [[(VECTOR, 256), (SCALAR, 256)]], multiply_tail, i)
+            if i == LAG - 1:
+                quantise_h()
+        for job in regrouped[-LAG:]:
+            quantise_and_multiply(job)
+        for m in range(TOKEN_TILES):
+            finish_tail(m)
+        for m in range(TOKEN_TILES):
+            store_tail(m)

@@ -26,18 +26,21 @@ D = 8192
 PASSES = D // K_PASS
 HEAD = 1024
 HEAD_TOKENS = 1022
+HEAD_BANKS = HEAD // BANK
 PROJ = 512
 TAIL = 2048
+TAIL_BANKS = TAIL // BANK
 
-BLOCKS = 2
-CHUNK = BLOCKS * BANK
-X_PASSES = 4
-LAG = 2
+CHUNK = 2 * BANK
+X_GROUP = 2
+RUN = 4
 PIECE = 256
 VECTOR, SCALAR, TENSOR = 0, 1, 2
-RUN = 4
 
-TAIL_BANK_ORDER = (0, 1, 2, 3, 7, 4, 5, 6)
+HEAD_STEPS = PASSES
+PROJ_STEPS = PASSES // 2
+STEPS = HEAD_STEPS + PROJ_STEPS + TAIL_BANKS
+PREFETCH = 7
 
 FLOPS = 2 * TOKENS * D * (HEAD + PROJ) + 2 * TOKENS * PROJ * TAIL
 
@@ -48,174 +51,268 @@ def tile_adaptiveinputsoftmax_pa_k_kernel(
     nc = tc.nc
     with ExitStack() as ctx:
         keep = ctx.enter_context(tc.tile_pool(name="keep", bufs=1))
-        x_pool = ctx.enter_context(tc.tile_pool(name="x_pool", bufs=4))
-        x_grouped_pool = ctx.enter_context(tc.tile_pool(name="x_grouped_pool", bufs=2))
-        wide_pool = ctx.enter_context(tc.tile_pool(name="wide_pool", bufs=6))
-        narrow_pool = ctx.enter_context(tc.tile_pool(name="narrow_pool", bufs=12))
-        grouped_pool = ctx.enter_context(tc.tile_pool(name="grouped_pool", bufs=LAG + 2))
-        codes_pool = ctx.enter_context(tc.tile_pool(name="codes_pool", bufs=3))
+        x_pool = ctx.enter_context(tc.tile_pool(name="x_pool", bufs=5))
+        x_grouped_pool = ctx.enter_context(tc.tile_pool(name="x_grouped_pool", bufs=3))
+        raw_pool = ctx.enter_context(tc.tile_pool(name="raw_pool", bufs=PREFETCH + 1))
+        half_pool = ctx.enter_context(tc.tile_pool(name="half_pool", bufs=TAIL_BANKS))
+        grouped_pool = ctx.enter_context(tc.tile_pool(name="grouped_pool", bufs=5))
+        codes_pool = ctx.enter_context(tc.tile_pool(name="codes_pool", bufs=5))
         psum = ctx.enter_context(tc.psum_pool(name="psum", bufs=1))
+        ctx.enter_context(tc.manual_schedule())
 
         def bank(index, name):
             return psum.tile([P, BANK], F32, tag="bank%d" % index, name=name)[:]
 
-        identity = keep.tile([P, P], F32, name="identity")
-        make_identity(nc, identity[:])
-        identity_bf16 = keep.tile([P, P], BF16, name="identity_bf16")
-        make_identity(nc, identity_bf16[:])
+        def stats(name, width):
+            return [keep.tile([P, width], F32, name=name + str(m)) for m in range(TOKEN_TILES)]
+
+        raws = {}
+        x_raws = {}
+
+        def load_weight(s):
+            if s == 0:
+                raws[s] = []
+                for first in range(0, HEAD, BANK):
+                    half = half_pool.tile([P, PACK, BANK], BF16, name="half")
+                    nc.sync.dma_start(
+                        out=half[:],
+                        in_=head_weight[0:K_PASS, first : first + BANK].rearrange(
+                            "(p t) w -> p t w", t=PACK
+                        ),
+                    )
+                    raws[s].append(half[:])
+            elif s < HEAD_STEPS:
+                raw = raw_pool.tile([P, PACK, HEAD], BF16, tag="raw", name="raw")
+                nc.sync.dma_start(
+                    out=raw[:],
+                    in_=head_weight[K_PASS * s : K_PASS * (s + 1), :].rearrange(
+                        "(p t) w -> p t w", t=PACK
+                    ),
+                )
+                raws[s] = [raw[:]]
+            elif s < HEAD_STEPS + PROJ_STEPS:
+                first = 2 * K_PASS * (s - HEAD_STEPS)
+                raw = raw_pool.tile([P, 2, PACK, PROJ], BF16, tag="raw", name="raw")
+                nc.sync.dma_start(
+                    out=raw[:],
+                    in_=tail_proj_0[first : first + 2 * K_PASS, :].rearrange(
+                        "(b p t) w -> p b t w", b=2, t=PACK
+                    ),
+                )
+                raws[s] = [raw[:, b] for b in range(2)]
+            else:
+                first = BANK * (s - HEAD_STEPS - PROJ_STEPS)
+                half = half_pool.tile([P, PACK, BANK], BF16, name="half")
+                nc.sync.dma_start(
+                    out=half[:],
+                    in_=tail_w_0[:, first : first + BANK].rearrange("(p t) w -> p t w", t=PACK),
+                )
+                raws[s] = [half[:]]
+
+        def load_x(group):
+            columns = slice(X_GROUP * K_PASS * group, X_GROUP * K_PASS * (group + 1))
+            raw = x_pool.tile([P, TOKEN_TILES, X_GROUP * K_PASS], BF16, name="x_raw")
+            nc.sync.dma_start(out=raw[:], in_=x[:, :, columns].rearrange("m r k -> r m k"))
+            x_raws[group] = raw
+
+        def load(s):
+            if s >= STEPS:
+                return
+            load_weight(s)
+            if s % X_GROUP == 1 and s < HEAD_STEPS:
+                load_x(s // X_GROUP)
+
+        for s in range(PREFETCH):
+            load(s)
+
         zero = keep.tile([P, 1], F32, name="zero")
         one = keep.tile([P, 1], F32, name="one")
         nc.vector.memset(zero[:], 0.0)
         nc.scalar.activation(out=one[:], in_=zero[:], func=EXP)
+        identity = keep.tile([P, P], F32, name="identity")
+        make_identity(nc, identity[:])
+        identity_bf16 = keep.tile([P, P], BF16, name="identity_bf16")
+        make_identity(nc, identity_bf16[:])
         cluster1 = keep.tile([P, P], F32, name="cluster1")
         nc.vector.memset(cluster1[:], 0.0)
 
         x_codes = keep.tile([P, PASSES * TOKENS], U32, align_bytes=64, name="x_codes")
         x_scales = keep.tile([P, PASSES * TOKENS], U8, align_bytes=64, name="x_scales")
+        x_transposed = {}
+        x_grouped = {}
 
-        def transpose_x(a):
-            columns = slice(X_PASSES * K_PASS * a, X_PASSES * K_PASS * (a + 1))
-            words = []
-            for m in range(TOKEN_TILES):
-                x_raw = x_pool.tile([P, X_PASSES * K_PASS], BF16, name="x_raw")
-                nc.sync.dma_start(out=x_raw[:], in_=x[m, :, columns])
-                words.append(
-                    x_raw[:].bitcast(F32).rearrange("r (g p u) -> r g u p", g=X_PASSES, u=2)
+        def transpose_rows(words, target):
+            for u in range(2):
+                for m in range(TOKEN_TILES):
+                    nc.tensor.transpose(
+                        target[:, u, P * m : P * (m + 1)], words[m][:, u, :], identity[:]
+                    )
+
+        def transpose_x(c):
+            raw = x_raws[c // X_GROUP]
+            columns = slice(K_PASS * (c % X_GROUP), K_PASS * (c % X_GROUP + 1))
+            words = [
+                raw[:, m, columns].bitcast(F32).rearrange("r (p u) -> r u p", u=2)
+                for m in range(TOKEN_TILES)
+            ]
+            x_transposed[c] = bank(4 + c % 2, "xt").rearrange("p (u r) -> p u r", u=2)
+            transpose_rows(words, x_transposed[c])
+
+        def copy_x(c):
+            if c % X_GROUP == 0:
+                x_grouped[c // X_GROUP] = x_grouped_pool.tile(
+                    [P, X_GROUP * TOKENS * PACK], BF16, align_bytes=64, name="x_grouped"
                 )
-            x_grouped = x_grouped_pool.tile(
-                [P, X_PASSES * TOKENS * PACK], BF16, align_bytes=64, name="x_grouped"
+            words = x_grouped[c // X_GROUP][:].bitcast(F32).rearrange(
+                "p (g r u) -> p g r u", g=X_GROUP, u=2
             )
-            grouped_words = x_grouped[:].bitcast(F32).rearrange(
-                "p (g r u) -> p g r u", g=X_PASSES, u=2
+            nc.scalar.copy(
+                out=words[:, c % X_GROUP], in_=x_transposed[c].rearrange("p u r -> p r u")
             )
-            for g in range(X_PASSES):
-                xt = bank(4 + (X_PASSES * a + g) % 3, "xt").rearrange("p (u r) -> p u r", u=2)
-                for u in range(2):
-                    for m in range(TOKEN_TILES):
-                        nc.tensor.transpose(
-                            xt[:, u, P * m : P * (m + 1)], words[m][:, g, u, :], identity[:]
-                        )
-                nc.scalar.copy(out=grouped_words[:, g], in_=xt.rearrange("p u r -> p r u"))
-            return x_grouped
 
-        def quantise_x(a, x_grouped):
-            columns = slice(X_PASSES * TOKENS * a, X_PASSES * TOKENS * (a + 1))
+        def quantise_x(group):
+            columns = slice(X_GROUP * TOKENS * group, X_GROUP * TOKENS * (group + 1))
             nc.vector.quantize_mx(
                 out=x_codes[:, columns].bitcast(FP8X4),
                 scales=x_scales[:, columns],
-                in_=x_grouped[:],
+                in_=x_grouped[group][:],
             )
 
-        regrouped = []
+        grouped = {}
+        identity_banks = {}
 
-        def quantise_and_multiply(job):
-            grouped, width, multiply, index = job
-            codes = codes_pool.tile([P, CHUNK], U32, align_bytes=64, name="codes")[:, 0:width]
-            scales = codes_pool.tile([P, CHUNK], U8, align_bytes=64, name="scales")[:, 0:width]
-            nc.vector.quantize_mx(
-                out=codes.bitcast(FP8X4),
-                scales=scales,
-                in_=grouped[:, 0:width, :].rearrange("p w t -> p (w t)"),
-            )
-            multiply(index, codes, scales)
+        def shares(s):
+            if s == 0:
+                return [[(VECTOR, 256), (SCALAR, 256)]] * 2
+            if s < HEAD_STEPS:
+                if s % 4 == 0:
+                    return [[(VECTOR, 512), (SCALAR, 512)]]
+                return [[(VECTOR, 512), (SCALAR, 256), (TENSOR, PIECE)]]
+            if s < HEAD_STEPS + PROJ_STEPS:
+                return [[(VECTOR, 384), (SCALAR, 128)], [(SCALAR, 256), (TENSOR, PIECE)]]
+            return [[(VECTOR, 256), (SCALAR, 256)]]
+
+        def parts(s, who):
+            found = []
+            width = 0
+            for raw, block in zip(raws[s], shares(s)):
+                first = 0
+                for engine, columns in block:
+                    if engine == who:
+                        source = raw[:, :, first : first + columns]
+                        found.append((source, slice(width, width + columns)))
+                    first += columns
+                    width += columns
+            return found
 
         def interleaved(view):
             return view.rearrange("p (c i) t -> p c t i", i=RUN)
 
-        def regroup(engine, target, source):
-            if engine == TENSOR:
-                bank7 = psum.tile([P, PIECE, PACK], BF16, tag="bank7", name="bank7")
+        def by_rows(view):
+            return view.rearrange("p t (c i) -> p c t i", i=RUN)
+
+        def identity_matmuls(s):
+            for source, target in parts(s, TENSOR):
+                identity_banks[s] = psum.tile(
+                    [P, PIECE, PACK], BF16, tag="bank%d" % (6 + s % 2), name="identity_bank"
+                )
                 for first in range(0, PIECE, P):
                     columns = slice(first, first + P)
                     nc.tensor.matmul(
-                        out=interleaved(bank7[:, columns, :]),
+                        out=interleaved(identity_banks[s][:, columns, :]),
                         lhsT=identity_bf16[:],
-                        rhs=source[:, :, columns].rearrange("p t (c i) -> p c t i", i=RUN),
+                        rhs=by_rows(source[:, :, columns]),
                         start=True,
                         stop=True,
                     )
-                nc.scalar.copy(out=target, in_=bank7[:])
-            else:
-                copy = nc.vector.tensor_copy if engine == VECTOR else nc.scalar.copy
-                copy(
-                    out=interleaved(target), in_=source.rearrange("p t (c i) -> p c t i", i=RUN)
+
+        def regroup(s, who):
+            if s not in grouped:
+                grouped[s] = grouped_pool.tile(
+                    [P, CHUNK, PACK], BF16, align_bytes=64, name="grouped"
                 )
+            for source, columns in parts(s, who):
+                target = grouped[s][:, columns, :]
+                if who == VECTOR:
+                    nc.vector.tensor_copy(out=interleaved(target), in_=by_rows(source))
+                elif who == SCALAR:
+                    nc.scalar.copy(out=interleaved(target), in_=by_rows(source))
+                else:
+                    nc.scalar.copy(out=target, in_=identity_banks[s][:])
 
-        def step(rows, shares, multiply, index):
-            grouped = grouped_pool.tile([P, CHUNK, PACK], BF16, align_bytes=64, name="grouped")
-            width = 0
-            for view, parts in zip(rows, shares):
-                first = 0
-                for engine, columns in parts:
-                    regroup(
-                        engine,
-                        grouped[:, width : width + columns, :],
-                        view[:, :, first : first + columns],
-                    )
-                    first += columns
-                    width += columns
-            regrouped.append((grouped, width, multiply, index))
-            if len(regrouped) > LAG:
-                quantise_and_multiply(regrouped[-1 - LAG])
+        codes = {}
 
-        def load(source):
-            width = source.shape[1]
-            pool = wide_pool if width == HEAD else narrow_pool
-            raw = pool.tile([P, PACK, width], BF16, name="raw")
-            nc.sync.dma_start(out=raw[:], in_=source.rearrange("(p t) w -> p t w", t=PACK))
-            return raw[:]
+        def quantise(s):
+            width = sum(columns for block in shares(s) for engine, columns in block)
+            code = codes_pool.tile([P, CHUNK], U32, align_bytes=64, name="code")
+            scale = codes_pool.tile([P, CHUNK], U8, align_bytes=64, name="scale")
+            codes[s] = (code[:, 0:width], scale[:, 0:width])
+            nc.vector.quantize_mx(
+                out=codes[s][0].bitcast(FP8X4),
+                scales=codes[s][1],
+                in_=grouped[s][:, 0:width, :].rearrange("p w t -> p (w t)"),
+            )
 
-        def multiply_pass(out, c, m, codes, scales, columns, start, stop):
-            tokens = slice(TOKENS * c + P * m, TOKENS * c + P * (m + 1))
+        def multiply_pass(out, left, left_columns, right, right_columns, start, stop):
             nc.tensor.matmul_mx(
                 out=out,
-                lhsT=x_codes[:, tokens].bitcast(FP8X4),
-                lhsT_scale=x_scales[:, tokens],
-                rhs=codes[:, columns].bitcast(FP8X4),
-                rhs_scale=scales[:, columns],
+                lhsT=left[0][:, left_columns].bitcast(FP8X4),
+                lhsT_scale=left[1][:, left_columns],
+                rhs=right[0][:, right_columns].bitcast(FP8X4),
+                rhs_scale=right[1][:, right_columns],
                 start=start,
                 stop=stop,
             )
 
-        HEAD_BANKS = HEAD // BANK
-        head_acc = [
-            [bank(HEAD_BANKS * m + n, "head_acc%d%d" % (m, n)) for n in range(HEAD_BANKS)]
-            for m in range(TOKEN_TILES)
-        ]
+        head_acc = []
+        h_acc = []
+        tail_logits = {}
+        TAIL_BANK_ORDER = (0, 1, 2, 4, 5, 3, 6, 7)
 
-        def multiply_head(c, codes, scales):
-            for m in range(TOKEN_TILES):
-                for n in range(HEAD_BANKS):
-                    columns = slice(BANK * n, BANK * (n + 1))
+        def x_tokens(c, m):
+            return slice(TOKENS * c + P * m, TOKENS * c + P * (m + 1))
+
+        def multiply(s):
+            if s == 0:
+                for m in range(TOKEN_TILES):
+                    head_acc.append(
+                        [bank(HEAD_BANKS * m + n, "head_acc") for n in range(HEAD_BANKS)]
+                    )
+            if s < HEAD_STEPS:
+                for m in range(TOKEN_TILES):
+                    for n in range(HEAD_BANKS):
+                        multiply_pass(
+                            head_acc[m][n], (x_codes, x_scales), x_tokens(s, m),
+                            codes[s], slice(BANK * n, BANK * (n + 1)),
+                            s == 0, s == PASSES - 1,
+                        )
+            elif s < HEAD_STEPS + PROJ_STEPS:
+                if s == HEAD_STEPS:
+                    h_acc.extend([bank(4 + m, "h_acc") for m in range(TOKEN_TILES)])
+                for b in range(2):
+                    c = 2 * (s - HEAD_STEPS) + b
+                    for m in range(TOKEN_TILES):
+                        multiply_pass(
+                            h_acc[m], (x_codes, x_scales), x_tokens(c, m),
+                            codes[s], slice(BANK * b, BANK * (b + 1)),
+                            c == 0, c == PASSES - 1,
+                        )
+            else:
+                n = s - HEAD_STEPS - PROJ_STEPS
+                for m in range(TOKEN_TILES):
+                    tail_logits[(m, n)] = bank(TAIL_BANK_ORDER[TOKEN_TILES * n + m], "tail_logits")
                     multiply_pass(
-                        head_acc[m][n], c, m, codes, scales, columns, c == 0, c == PASSES - 1
+                        tail_logits[(m, n)], (h_codes, h_scales), slice(P * m, P * (m + 1)),
+                        codes[s], slice(0, BANK), True, True,
                     )
 
-        for c in range(PASSES):
-            weight = head_weight[K_PASS * c : K_PASS * (c + 1), :]
-            if c == 0:
-                rows = [load(weight[:, 0:BANK]), load(weight[:, BANK:HEAD])]
-                shares = [[(VECTOR, 256), (SCALAR, 256)], [(VECTOR, 256), (TENSOR, 256)]]
-            else:
-                rows = [load(weight)]
-                shares = [[(SCALAR, 256), (VECTOR, 512), (TENSOR, 256)]]
-            step(rows, shares, multiply_head, c)
-            if c % X_PASSES == 0:
-                x_grouped = transpose_x(c // X_PASSES)
-            if c % X_PASSES == 1:
-                quantise_x(c // X_PASSES, x_grouped)
-
-        head_exp = [keep.tile([P, HEAD], F32, name="head_exp%d" % m) for m in range(TOKEN_TILES)]
-        head_bank_max = [
-            keep.tile([P, HEAD_BANKS], F32, name="head_bank_max%d" % m) for m in range(TOKEN_TILES)
-        ]
-        head_neg_max = [keep.tile([P, 1], F32, name="head_neg_max%d" % m) for m in range(TOKEN_TILES)]
-        head_bank_sum = [
-            keep.tile([P, HEAD_BANKS], F32, name="head_bank_sum%d" % m) for m in range(TOKEN_TILES)
-        ]
-        head_sum = [keep.tile([P, 1], F32, name="head_sum%d" % m) for m in range(TOKEN_TILES)]
-        head_inverse = [keep.tile([P, 1], F32, name="head_inverse%d" % m) for m in range(TOKEN_TILES)]
-        cluster0 = [keep.tile([P, 1], F32, name="cluster0_%d" % m) for m in range(TOKEN_TILES)]
+        head_exp = stats("head_exp", HEAD)
+        head_bank_max = stats("head_bank_max", HEAD_BANKS)
+        head_neg_max = stats("head_neg_max", 1)
+        head_bank_sum = stats("head_bank_sum", HEAD_BANKS)
+        head_sum = stats("head_sum", 1)
+        head_inverse = stats("head_inverse", 1)
+        cluster0 = stats("cluster0_", 1)
 
         def max_head(m):
             for n in range(HEAD_BANKS):
@@ -236,7 +333,7 @@ def tile_adaptiveinputsoftmax_pa_k_kernel(
                     accum_out=head_bank_sum[m][:, n : n + 1],
                 )
 
-        def finish_head(m):
+        def normalise_head(m):
             nc.vector.reduce_sum(out=head_sum[m][:], in_=head_bank_sum[m][:], axis=ALONG_ROW)
             nc.vector.reciprocal(out=head_inverse[m][:], in_=head_sum[m][:])
             for column, target in ((0, cluster0[m][:]), (1, cluster1[:, m : m + 1])):
@@ -254,72 +351,52 @@ def tile_adaptiveinputsoftmax_pa_k_kernel(
                 scalar2=None,
                 op0=MULT,
             )
+
+        def store_head(m):
             nc.sync.dma_start(out=out_0[m, :, 0:HEAD_TOKENS], in_=head_exp[m][:, 0:HEAD_TOKENS])
 
+        cluster1_out = keep.tile([P, P], F32, name="cluster1_out")
+
+        def turn_cluster1():
+            rows = bank(2, "cluster1_rows")
+            nc.tensor.transpose(rows[:, 0:P], cluster1[:], identity[:])
+            nc.scalar.copy(out=cluster1_out[:], in_=rows[:, 0:P])
+
         def store_cluster1():
-            cluster1_rows = bank(7, "cluster1_rows")
-            nc.tensor.transpose(cluster1_rows[:, 0:P], cluster1[:], identity[:])
-            cluster1_out = keep.tile([P, P], F32, name="cluster1_out")
-            nc.scalar.copy(out=cluster1_out[:], in_=cluster1_rows[:, 0:P])
             nc.sync.dma_start(
                 out=out_1.rearrange("n t o -> n (t o)"), in_=cluster1_out[0:TOKEN_TILES, :]
             )
 
-        head_stages = [stage for m in range(TOKEN_TILES) for stage in (
-            lambda m=m: max_head(m), lambda m=m: exp_head(m), lambda m=m: finish_head(m)
-        )]
-        head_stages.append(store_cluster1)
-
-        h_acc = [bank(4 + m, "h_acc%d" % m) for m in range(TOKEN_TILES)]
-
-        def project(j, codes, scales):
-            for b in range(BLOCKS):
-                c = BLOCKS * j + b
-                columns = slice(BANK * b, BANK * (b + 1))
-                for m in range(TOKEN_TILES):
-                    multiply_pass(h_acc[m], c, m, codes, scales, columns, c == 0, c == PASSES - 1)
-
-        for j in range(PASSES // BLOCKS):
-            rows = [
-                load(tail_proj_0[K_PASS * c : K_PASS * (c + 1), :])
-                for c in range(BLOCKS * j, BLOCKS * (j + 1))
-            ]
-            step(rows, [[(VECTOR, 256), (SCALAR, 256)]] * BLOCKS, project, j)
-            if LAG - 1 <= j < LAG - 1 + len(head_stages):
-                head_stages[j - LAG + 1]()
-
         h_rounded = [keep.tile([P, PROJ], BF16, name="h_rounded%d" % m) for m in range(TOKEN_TILES)]
-        h_grouped = keep.tile([P, TOKENS, PACK], BF16, align_bytes=64, name="h_grouped")
+        h_grouped = keep.tile([P, TOKENS * PACK], BF16, align_bytes=64, name="h_grouped")
         h_codes = keep.tile([P, TOKENS], U32, align_bytes=64, name="h_codes")
         h_scales = keep.tile([P, TOKENS], U8, align_bytes=64, name="h_scales")
+        h_transposed = []
+
+        def round_h():
+            nc.vector.tensor_copy(out=h_rounded[0][:], in_=h_acc[0])
+            nc.scalar.copy(out=h_rounded[1][:], in_=h_acc[1])
+
+        def transpose_h():
+            h_transposed.append(bank(3, "ht").rearrange("p (u r) -> p u r", u=2))
+            words = [
+                h_rounded[m][:].bitcast(F32).rearrange("r (p u) -> r u p", u=2)
+                for m in range(TOKEN_TILES)
+            ]
+            transpose_rows(words, h_transposed[0])
+
+        def copy_h():
+            nc.scalar.copy(
+                out=h_grouped[:].bitcast(F32).rearrange("p (r u) -> p r u", u=2),
+                in_=h_transposed[0].rearrange("p u r -> p r u"),
+            )
 
         def quantise_h():
-            for m in range(TOKEN_TILES):
-                copy = nc.vector.tensor_copy if m == 0 else nc.scalar.copy
-                copy(out=h_rounded[m][:], in_=h_acc[m])
-            ht = bank(6, "ht").rearrange("p (u r) -> p u r", u=2)
-            for u in range(2):
-                for m in range(TOKEN_TILES):
-                    words = h_rounded[m][:].bitcast(F32).rearrange("r (p u) -> r u p", u=2)
-                    nc.tensor.transpose(ht[:, u, P * m : P * (m + 1)], words[:, u, :], identity[:])
-            nc.vector.tensor_copy(
-                out=h_grouped[:].rearrange("p r t -> p (r t)").bitcast(F32).rearrange(
-                    "p (r u) -> p r u", u=2
-                ),
-                in_=ht.rearrange("p u r -> p r u"),
-            )
             nc.vector.quantize_mx(
-                out=h_codes[:].bitcast(FP8X4),
-                scales=h_scales[:],
-                in_=h_grouped[:].rearrange("p r t -> p (r t)"),
+                out=h_codes[:].bitcast(FP8X4), scales=h_scales[:], in_=h_grouped[:]
             )
 
-        TAIL_BANKS = TAIL // BANK
-        tail_exp = [keep.tile([P, TAIL], F32, name="tail_exp%d" % m) for m in range(TOKEN_TILES)]
-
-        def stats(name, width):
-            return [keep.tile([P, width], F32, name=name + str(m)) for m in range(TOKEN_TILES)]
-
+        tail_exp = stats("tail_exp", TAIL)
         bank_neg_max = stats("bank_neg_max", TAIL_BANKS)
         bank_sum = stats("bank_sum", TAIL_BANKS)
         tail_neg_max = stats("tail_neg_max", 1)
@@ -329,40 +406,23 @@ def tile_adaptiveinputsoftmax_pa_k_kernel(
         tail_inverse = stats("tail_inverse", 1)
         bank_scale = stats("bank_scale", TAIL_BANKS)
 
-        def multiply_tail(first_bank, codes, scales):
-            for i in range(codes.shape[1] // BANK):
-                n = first_bank + i
-                columns = slice(BANK * i, BANK * (i + 1))
-                logits = []
-                for m in range(TOKEN_TILES):
-                    tokens = slice(P * m, P * (m + 1))
-                    logits.append(bank(TAIL_BANK_ORDER[TOKEN_TILES * n + m], "tail_logits"))
-                    nc.tensor.matmul_mx(
-                        out=logits[m],
-                        lhsT=h_codes[:, tokens].bitcast(FP8X4),
-                        lhsT_scale=h_scales[:, tokens],
-                        rhs=codes[:, columns].bitcast(FP8X4),
-                        rhs_scale=scales[:, columns],
-                        start=True,
-                        stop=True,
-                    )
-                for m in range(TOKEN_TILES):
-                    nc.vector.tensor_reduce(
-                        out=bank_neg_max[m][:, n : n + 1],
-                        in_=logits[m],
-                        axis=ALONG_ROW,
-                        op=MAX,
-                        negate=True,
-                    )
-                    nc.scalar.activation(
-                        out=tail_exp[m][:, BANK * n : BANK * (n + 1)],
-                        in_=logits[m],
-                        func=EXP,
-                        bias=bank_neg_max[m][:, n : n + 1],
-                        accum_out=bank_sum[m][:, n : n + 1],
-                    )
+        def softmax_bank(n, m):
+            nc.vector.tensor_reduce(
+                out=bank_neg_max[m][:, n : n + 1],
+                in_=tail_logits[(m, n)],
+                axis=ALONG_ROW,
+                op=MAX,
+                negate=True,
+            )
+            nc.scalar.activation(
+                out=tail_exp[m][:, BANK * n : BANK * (n + 1)],
+                in_=tail_logits[(m, n)],
+                func=EXP,
+                bias=bank_neg_max[m][:, n : n + 1],
+                accum_out=bank_sum[m][:, n : n + 1],
+            )
 
-        def finish_tail(m):
+        def tail_factors(m):
             nc.vector.tensor_reduce(
                 out=tail_neg_max[m][:], in_=bank_neg_max[m][:], axis=ALONG_ROW, op=MIN
             )
@@ -373,6 +433,8 @@ def tile_adaptiveinputsoftmax_pa_k_kernel(
                 scale=-1.0,
                 bias=tail_neg_max[m][:],
             )
+
+        def tail_scales(m):
             nc.vector.tensor_tensor(
                 out=scaled_sum[m][:], in0=bank_factor[m][:], in1=bank_sum[m][:], op=MULT
             )
@@ -410,14 +472,67 @@ def tile_adaptiveinputsoftmax_pa_k_kernel(
                     in_=tail_exp[m][:, columns],
                 )
 
-        for i in range(TAIL_BANKS):
-            columns = slice(BANK * i, BANK * (i + 1))
-            step([load(tail_w_0[:, columns])], [[(VECTOR, 256), (SCALAR, 256)]], multiply_tail, i)
-            if i == LAG - 1:
-                quantise_h()
-        for job in regrouped[-LAG:]:
-            quantise_and_multiply(job)
+        first_tail = HEAD_STEPS + PROJ_STEPS
+        quantised_in = {s: [s - 2] for s in range(2, first_tail - 1)}
+        quantised_in[first_tail - 1] = [first_tail - 3, first_tail - 2]
+        quantised_in[first_tail] = [first_tail - 1]
+        quantised_in[first_tail + 1] = [first_tail]
+        quantised_in[first_tail + 2] = [first_tail + 1]
+        multiplied_in = {s: [s - 4] for s in range(4, HEAD_STEPS + 4)}
+        multiplied_in[HEAD_STEPS + 4] = [HEAD_STEPS, HEAD_STEPS + 1]
+        for s in range(HEAD_STEPS + 5, first_tail):
+            multiplied_in[s] = [s - 3]
+        multiplied_in[first_tail] = [first_tail - 3, first_tail - 2, first_tail - 1]
+        softmax_step = HEAD_STEPS + 4
+
+        identity_matmuls(0)
+        for s in range(STEPS):
+            load(s + PREFETCH)
+            if s > softmax_step + 2:
+                pass_over = s - softmax_step - 3
+                if pass_over < TOKEN_TILES:
+                    store_head(pass_over)
+            if s + 1 < STEPS:
+                identity_matmuls(s + 1)
+            if s < PASSES:
+                transpose_x(s)
+            if s == softmax_step + 1:
+                exp_head(0)
+            if s == softmax_step + 2:
+                exp_head(1)
+            regroup(s, VECTOR)
+            regroup(s, SCALAR)
+            if 1 <= s <= PASSES:
+                copy_x(s - 1)
+            regroup(s, TENSOR)
+            if s % X_GROUP == 1 and 3 <= s <= PASSES + 1:
+                quantise_x((s - 3) // X_GROUP)
+            for job in quantised_in.get(s, []):
+                quantise(job)
+            for job in multiplied_in.get(s, []):
+                multiply(job)
+            if s in (softmax_step, softmax_step + 1):
+                max_head(s - softmax_step)
+            if s in (softmax_step + 2, softmax_step + 3):
+                normalise_head(s - softmax_step - 2)
+            if s == first_tail:
+                turn_cluster1()
+            if s == first_tail + 1:
+                store_cluster1()
+                round_h()
+                transpose_h()
+            if s == first_tail + 2:
+                copy_h()
+        quantise_h()
+        quantise(first_tail + 2)
+        for n in range(TAIL_BANKS):
+            if n == 2:
+                quantise(first_tail + 3)
+            multiply(first_tail + n)
+            for m in range(TOKEN_TILES):
+                softmax_bank(n, m)
+                if n == TAIL_BANKS - 1:
+                    tail_factors(m)
         for m in range(TOKEN_TILES):
-            finish_tail(m)
-        for m in range(TOKEN_TILES):
+            tail_scales(m)
             store_tail(m)

@@ -13,6 +13,7 @@ COPY = mybir.ActivationFunctionType.Copy
 MULT = mybir.AluOpType.mult
 MAX = mybir.AluOpType.max
 MIN = mybir.AluOpType.min
+ADD = mybir.AluOpType.add
 ALONG_ROW = mybir.AxisListType.X
 
 P = 128
@@ -41,6 +42,7 @@ HEAD_STEPS = PASSES
 PROJ_STEPS = PASSES // 2
 STEPS = HEAD_STEPS + PROJ_STEPS + TAIL_BANKS
 PREFETCH = 7
+X_DELAY = 2
 
 FLOPS = 2 * TOKENS * D * (HEAD + PROJ) + 2 * TOKENS * PROJ * TAIL
 
@@ -55,8 +57,8 @@ def tile_adaptiveinputsoftmax_pa_k_kernel(
         x_grouped_pool = ctx.enter_context(tc.tile_pool(name="x_grouped_pool", bufs=3))
         raw_pool = ctx.enter_context(tc.tile_pool(name="raw_pool", bufs=PREFETCH + 1))
         half_pool = ctx.enter_context(tc.tile_pool(name="half_pool", bufs=TAIL_BANKS))
-        grouped_pool = ctx.enter_context(tc.tile_pool(name="grouped_pool", bufs=5))
-        codes_pool = ctx.enter_context(tc.tile_pool(name="codes_pool", bufs=5))
+        grouped_pool = ctx.enter_context(tc.tile_pool(name="grouped_pool", bufs=4))
+        codes_pool = ctx.enter_context(tc.tile_pool(name="codes_pool", bufs=7))
         psum = ctx.enter_context(tc.psum_pool(name="psum", bufs=1))
         ctx.enter_context(tc.manual_schedule())
 
@@ -119,8 +121,8 @@ def tile_adaptiveinputsoftmax_pa_k_kernel(
             if s >= STEPS:
                 return
             load_weight(s)
-            if s % X_GROUP == 1 and s < HEAD_STEPS:
-                load_x(s // X_GROUP)
+            if s % X_GROUP == 0 and X_DELAY <= s < PASSES + X_DELAY:
+                load_x((s - X_DELAY) // X_GROUP)
 
         for s in range(PREFETCH):
             load(s)
@@ -187,7 +189,7 @@ def tile_adaptiveinputsoftmax_pa_k_kernel(
             if s < HEAD_STEPS:
                 if s % 4 == 0:
                     return [[(VECTOR, 512), (SCALAR, 512)]]
-                return [[(VECTOR, 512), (SCALAR, 256), (TENSOR, PIECE)]]
+                return [[(VECTOR, 384), (SCALAR, 384), (TENSOR, PIECE)]]
             if s < HEAD_STEPS + PROJ_STEPS:
                 return [[(VECTOR, 384), (SCALAR, 128)], [(SCALAR, 256), (TENSOR, PIECE)]]
             return [[(VECTOR, 256), (SCALAR, 256)]]
@@ -267,7 +269,7 @@ def tile_adaptiveinputsoftmax_pa_k_kernel(
         head_acc = []
         h_acc = []
         tail_logits = {}
-        TAIL_BANK_ORDER = (0, 1, 2, 4, 5, 3, 6, 7)
+        TAIL_BANK_ORDER = (0, 1, 2, 6, 7, 4, 5, 3)
 
         def x_tokens(c, m):
             return slice(TOKENS * c + P * m, TOKENS * c + P * (m + 1))
@@ -319,6 +321,8 @@ def tile_adaptiveinputsoftmax_pa_k_kernel(
                 nc.vector.reduce_max(
                     out=head_bank_max[m][:, n : n + 1], in_=head_acc[m][n], axis=ALONG_ROW
                 )
+
+        def join_head_max(m):
             nc.vector.tensor_reduce(
                 out=head_neg_max[m][:], in_=head_bank_max[m][:], axis=ALONG_ROW, op=MAX, negate=True
             )
@@ -333,34 +337,39 @@ def tile_adaptiveinputsoftmax_pa_k_kernel(
                     accum_out=head_bank_sum[m][:, n : n + 1],
                 )
 
-        def normalise_head(m):
+        def sum_head(m):
             nc.vector.reduce_sum(out=head_sum[m][:], in_=head_bank_sum[m][:], axis=ALONG_ROW)
+
+        def invert_head(m):
             nc.vector.reciprocal(out=head_inverse[m][:], in_=head_sum[m][:])
-            for column, target in ((0, cluster0[m][:]), (1, cluster1[:, m : m + 1])):
+
+        def scale_head(m):
+            for source, target in (
+                (slice(HEAD_TOKENS, HEAD_TOKENS + 1), cluster0[m][:]),
+                (slice(HEAD_TOKENS + 1, HEAD_TOKENS + 2), cluster1[:, m : m + 1]),
+                (slice(0, HEAD_TOKENS), head_exp[m][:, 0:HEAD_TOKENS]),
+            ):
                 nc.vector.tensor_scalar(
                     out=target,
-                    in0=head_exp[m][:, HEAD_TOKENS + column : HEAD_TOKENS + column + 1],
+                    in0=head_exp[m][:, source],
                     scalar1=head_inverse[m][:],
                     scalar2=None,
                     op0=MULT,
                 )
-            nc.vector.tensor_scalar(
-                out=head_exp[m][:, 0:HEAD_TOKENS],
-                in0=head_exp[m][:, 0:HEAD_TOKENS],
-                scalar1=head_inverse[m][:],
-                scalar2=None,
-                op0=MULT,
-            )
 
         def store_head(m):
             nc.sync.dma_start(out=out_0[m, :, 0:HEAD_TOKENS], in_=head_exp[m][:, 0:HEAD_TOKENS])
 
+        cluster1_rows = []
         cluster1_out = keep.tile([P, P], F32, name="cluster1_out")
 
         def turn_cluster1():
             rows = bank(2, "cluster1_rows")
             nc.tensor.transpose(rows[:, 0:P], cluster1[:], identity[:])
-            nc.scalar.copy(out=cluster1_out[:], in_=rows[:, 0:P])
+            cluster1_rows.append(rows)
+
+        def copy_cluster1():
+            nc.scalar.copy(out=cluster1_out[:], in_=cluster1_rows[0][:, 0:P])
 
         def store_cluster1():
             nc.sync.dma_start(
@@ -396,17 +405,19 @@ def tile_adaptiveinputsoftmax_pa_k_kernel(
                 out=h_codes[:].bitcast(FP8X4), scales=h_scales[:], in_=h_grouped[:]
             )
 
+        LAST = TAIL_BANKS - 1
         tail_exp = stats("tail_exp", TAIL)
         bank_neg_max = stats("bank_neg_max", TAIL_BANKS)
         bank_sum = stats("bank_sum", TAIL_BANKS)
         tail_neg_max = stats("tail_neg_max", 1)
-        bank_factor = stats("bank_factor", TAIL_BANKS)
-        scaled_sum = stats("scaled_sum", TAIL_BANKS)
+        factor = stats("factor", TAIL_BANKS)
+        cluster_factor = stats("cluster_factor", TAIL_BANKS)
+        scaled_sum = stats("scaled_sum", LAST)
+        early_sum = stats("early_sum", 1)
         tail_sum = stats("tail_sum", 1)
         tail_inverse = stats("tail_inverse", 1)
-        bank_scale = stats("bank_scale", TAIL_BANKS)
 
-        def softmax_bank(n, m):
+        def max_bank(n, m):
             nc.vector.tensor_reduce(
                 out=bank_neg_max[m][:, n : n + 1],
                 in_=tail_logits[(m, n)],
@@ -414,6 +425,8 @@ def tile_adaptiveinputsoftmax_pa_k_kernel(
                 op=MAX,
                 negate=True,
             )
+
+        def exp_bank(n, m):
             nc.scalar.activation(
                 out=tail_exp[m][:, BANK * n : BANK * (n + 1)],
                 in_=tail_logits[(m, n)],
@@ -422,117 +435,159 @@ def tile_adaptiveinputsoftmax_pa_k_kernel(
                 accum_out=bank_sum[m][:, n : n + 1],
             )
 
-        def tail_factors(m):
+        def join_tail_max(m):
             nc.vector.tensor_reduce(
                 out=tail_neg_max[m][:], in_=bank_neg_max[m][:], axis=ALONG_ROW, op=MIN
             )
+
+        def exp_factor(m):
             nc.scalar.activation(
-                out=bank_factor[m][:],
+                out=factor[m][:],
                 in_=bank_neg_max[m][:],
                 func=EXP,
                 scale=-1.0,
                 bias=tail_neg_max[m][:],
             )
 
-        def tail_scales(m):
-            nc.vector.tensor_tensor(
-                out=scaled_sum[m][:], in0=bank_factor[m][:], in1=bank_sum[m][:], op=MULT
-            )
-            nc.vector.reduce_sum(out=tail_sum[m][:], in_=scaled_sum[m][:], axis=ALONG_ROW)
-            nc.vector.reciprocal(out=tail_inverse[m][:], in_=tail_sum[m][:])
+        def scale_factor(m):
             nc.vector.tensor_scalar(
-                out=bank_scale[m][:],
-                in0=bank_factor[m][:],
-                scalar1=tail_inverse[m][:],
-                scalar2=cluster0[m][:],
-                op0=MULT,
-                op1=MULT,
+                out=cluster_factor[m][:], in0=factor[m][:], scalar1=cluster0[m][:], scalar2=None, op0=MULT
             )
+
+        def scale_sums(m):
+            nc.vector.tensor_tensor(
+                out=scaled_sum[m][:], in0=factor[m][:, 0:LAST], in1=bank_sum[m][:, 0:LAST], op=MULT
+            )
+
+        def add_sums(m):
+            nc.vector.reduce_sum(out=early_sum[m][:], in_=scaled_sum[m][:], axis=ALONG_ROW)
+
+        def invert_sum(m):
+            nc.vector.scalar_tensor_tensor(
+                out=tail_sum[m][:],
+                in0=bank_sum[m][:, LAST:TAIL_BANKS],
+                scalar=factor[m][:, LAST:TAIL_BANKS],
+                in1=early_sum[m][:],
+                op0=MULT,
+                op1=ADD,
+            )
+            nc.vector.reciprocal(out=tail_inverse[m][:], in_=tail_sum[m][:])
 
         def store_tail(m):
             for n in range(TAIL_BANKS):
                 columns = slice(BANK * n, BANK * (n + 1))
-                if n == TAIL_BANKS - 1:
-                    nc.scalar.activation(
-                        out=tail_exp[m][:, columns],
-                        in_=tail_exp[m][:, columns],
-                        func=COPY,
-                        scale=bank_scale[m][:, n : n + 1],
-                    )
-                else:
-                    nc.vector.tensor_scalar(
-                        out=tail_exp[m][:, columns],
-                        in0=tail_exp[m][:, columns],
-                        scalar1=bank_scale[m][:, n : n + 1],
-                        scalar2=None,
-                        op0=MULT,
-                    )
+                nc.vector.tensor_scalar(
+                    out=tail_exp[m][:, columns],
+                    in0=tail_exp[m][:, columns],
+                    scalar1=cluster_factor[m][:, n : n + 1],
+                    scalar2=tail_inverse[m][:],
+                    op0=MULT,
+                    op1=MULT,
+                )
                 nc.sync.dma_start(
                     out=out_0[m, :, HEAD_TOKENS + BANK * n : HEAD_TOKENS + BANK * (n + 1)],
                     in_=tail_exp[m][:, columns],
                 )
 
         first_tail = HEAD_STEPS + PROJ_STEPS
-        quantised_in = {s: [s - 2] for s in range(2, first_tail - 1)}
+        quantised_in = {1: [0], 2: [1]}
+        for s in range(4, first_tail - 1):
+            quantised_in[s] = [s - 2]
         quantised_in[first_tail - 1] = [first_tail - 3, first_tail - 2]
-        quantised_in[first_tail] = [first_tail - 1]
-        quantised_in[first_tail + 1] = [first_tail]
-        quantised_in[first_tail + 2] = [first_tail + 1]
-        multiplied_in = {s: [s - 4] for s in range(4, HEAD_STEPS + 4)}
-        multiplied_in[HEAD_STEPS + 4] = [HEAD_STEPS, HEAD_STEPS + 1]
+        for s in range(first_tail, STEPS):
+            quantised_in[s] = [s - 1]
+        multiplied_in = {s: [s - 5] for s in range(5, HEAD_STEPS + 3)}
+        for i in range(2):
+            multiplied_in[HEAD_STEPS + 3 + i] = [HEAD_STEPS - 2 + 2 * i, HEAD_STEPS - 1 + 2 * i]
         for s in range(HEAD_STEPS + 5, first_tail):
             multiplied_in[s] = [s - 3]
         multiplied_in[first_tail] = [first_tail - 3, first_tail - 2, first_tail - 1]
         softmax_step = HEAD_STEPS + 4
+        before_regrouping = {
+            softmax_step + 1: lambda: join_head_max(0),
+            softmax_step + 2: lambda: join_head_max(1),
+            softmax_step + 3: lambda: scale_head(0),
+            softmax_step + 4: lambda: scale_head(1),
+        }
+        after_regrouping = {
+            softmax_step + 2: lambda: sum_head(0),
+            softmax_step + 3: lambda: sum_head(1),
+            first_tail + 3: quantise_h,
+        }
+        after_quantising = {
+            softmax_step: lambda: max_head(0),
+            softmax_step + 1: lambda: max_head(1),
+            softmax_step + 2: lambda: invert_head(0),
+            softmax_step + 3: lambda: invert_head(1),
+        }
 
         identity_matmuls(0)
         for s in range(STEPS):
             load(s + PREFETCH)
-            if s > softmax_step + 2:
-                pass_over = s - softmax_step - 3
-                if pass_over < TOKEN_TILES:
-                    store_head(pass_over)
+            if s in (softmax_step + 4, softmax_step + 5):
+                store_head(s - softmax_step - 4)
+            if s == STEPS - 1:
+                store_cluster1()
+            x_pass = s - X_DELAY
+            if 0 <= x_pass < PASSES:
+                transpose_x(x_pass)
             if s + 1 < STEPS:
                 identity_matmuls(s + 1)
-            if s < PASSES:
-                transpose_x(s)
-            if s == softmax_step + 1:
-                exp_head(0)
-            if s == softmax_step + 2:
-                exp_head(1)
-            regroup(s, VECTOR)
             regroup(s, SCALAR)
-            if 1 <= s <= PASSES:
-                copy_x(s - 1)
+            if 0 <= x_pass < PASSES:
+                copy_x(x_pass)
             regroup(s, TENSOR)
-            if s % X_GROUP == 1 and 3 <= s <= PASSES + 1:
-                quantise_x((s - 3) // X_GROUP)
-            for job in quantised_in.get(s, []):
-                quantise(job)
+            if s <= X_DELAY:
+                for job in quantised_in.get(s, []):
+                    quantise(job)
+            if s in before_regrouping:
+                before_regrouping[s]()
+            regroup(s, VECTOR)
+            if x_pass % X_GROUP == 0 and X_GROUP <= x_pass <= PASSES:
+                quantise_x(x_pass // X_GROUP - 1)
+            if s in after_regrouping:
+                after_regrouping[s]()
+            if s > X_DELAY:
+                for job in quantised_in.get(s, []):
+                    quantise(job)
+            if s in after_quantising:
+                after_quantising[s]()
+            if s in (softmax_step + 1, softmax_step + 2):
+                exp_head(s - softmax_step - 1)
             for job in multiplied_in.get(s, []):
                 multiply(job)
-            if s in (softmax_step, softmax_step + 1):
-                max_head(s - softmax_step)
-            if s in (softmax_step + 2, softmax_step + 3):
-                normalise_head(s - softmax_step - 2)
-            if s == first_tail:
-                turn_cluster1()
             if s == first_tail + 1:
-                store_cluster1()
                 round_h()
                 transpose_h()
+                turn_cluster1()
             if s == first_tail + 2:
                 copy_h()
-        quantise_h()
-        quantise(first_tail + 2)
+                copy_cluster1()
         for n in range(TAIL_BANKS):
-            if n == 2:
-                quantise(first_tail + 3)
+            if n == 1:
+                quantise(first_tail + LAST)
             multiply(first_tail + n)
-            for m in range(TOKEN_TILES):
-                softmax_bank(n, m)
-                if n == TAIL_BANKS - 1:
-                    tail_factors(m)
-        for m in range(TOKEN_TILES):
-            tail_scales(m)
-            store_tail(m)
+            max_bank(n, 0)
+            exp_bank(n, 0)
+        max_bank(0, 1)
+        join_tail_max(0)
+        exp_factor(0)
+        exp_bank(0, 1)
+        max_bank(1, 1)
+        exp_bank(1, 1)
+        scale_factor(0)
+        scale_sums(0)
+        max_bank(2, 1)
+        exp_bank(2, 1)
+        add_sums(0)
+        max_bank(3, 1)
+        invert_sum(0)
+        join_tail_max(1)
+        exp_factor(1)
+        exp_bank(3, 1)
+        store_tail(0)
+        scale_factor(1)
+        scale_sums(1)
+        add_sums(1)
+        invert_sum(1)
+        store_tail(1)

@@ -187,9 +187,7 @@ def tile_adaptiveinputsoftmax_pa_k_kernel(
             if s == 0:
                 return [[(VECTOR, 256), (SCALAR, 256)]] * 2
             if s < HEAD_STEPS:
-                if s % 4 == 0:
-                    return [[(VECTOR, 512), (SCALAR, 512)]]
-                return [[(VECTOR, 384), (SCALAR, 384), (TENSOR, PIECE)]]
+                return [[(VECTOR, 576), (SCALAR, 448)]]
             if s < HEAD_STEPS + PROJ_STEPS:
                 return [[(VECTOR, 384), (SCALAR, 128)], [(SCALAR, 256), (TENSOR, PIECE)]]
             return [[(VECTOR, 256), (SCALAR, 256)]]

@@ -38,11 +38,24 @@ RUN = 4
 PIECE = 256
 VECTOR, SCALAR, TENSOR = 0, 1, 2
 
-HEAD_STEPS = PASSES
-PROJ_STEPS = PASSES // 2
-STEPS = HEAD_STEPS + PROJ_STEPS + TAIL_BANKS
-PREFETCH = 7
-X_DELAY = 2
+GROUPS = PASSES // X_GROUP
+PROJ_KIND, HEAD_KIND, TAIL_KIND = 0, 1, 2
+
+CHUNKS = (
+    [(PROJ_KIND, 0)]
+    + [
+        chunk
+        for g in range(1, GROUPS)
+        for chunk in ((PROJ_KIND, g), (HEAD_KIND, 2 * g - 2), (HEAD_KIND, 2 * g - 1))
+    ]
+    + [(HEAD_KIND, PASSES - 2), (HEAD_KIND, PASSES - 1)]
+    + [(TAIL_KIND, n) for n in range(TAIL_BANKS)]
+)
+STEPS = len(CHUNKS)
+FIRST_TAIL = STEPS - TAIL_BANKS
+PROJ_STEPS = [s for s in range(STEPS) if CHUNKS[s][0] == PROJ_KIND]
+X_LOAD_STEPS = [PROJ_STEPS[0] + 1, PROJ_STEPS[1] + 1] + PROJ_STEPS[2:]
+PREFETCH = 6
 
 FLOPS = 2 * TOKENS * D * (HEAD + PROJ) + 2 * TOKENS * PROJ * TAIL
 
@@ -58,7 +71,7 @@ def tile_adaptiveinputsoftmax_pa_k_kernel(
         raw_pool = ctx.enter_context(tc.tile_pool(name="raw_pool", bufs=PREFETCH + 1))
         half_pool = ctx.enter_context(tc.tile_pool(name="half_pool", bufs=TAIL_BANKS))
         grouped_pool = ctx.enter_context(tc.tile_pool(name="grouped_pool", bufs=4))
-        codes_pool = ctx.enter_context(tc.tile_pool(name="codes_pool", bufs=7))
+        codes_pool = ctx.enter_context(tc.tile_pool(name="codes_pool", bufs=6))
         psum = ctx.enter_context(tc.psum_pool(name="psum", bufs=1))
         ctx.enter_context(tc.manual_schedule())
 
@@ -72,44 +85,39 @@ def tile_adaptiveinputsoftmax_pa_k_kernel(
         x_raws = {}
 
         def load_weight(s):
-            if s == 0:
-                raws[s] = []
-                for first in range(0, HEAD, BANK):
-                    half = half_pool.tile([P, PACK, BANK], BF16, name="half")
-                    nc.sync.dma_start(
-                        out=half[:],
-                        in_=head_weight[0:K_PASS, first : first + BANK].rearrange(
-                            "(p t) w -> p t w", t=PACK
-                        ),
-                    )
-                    raws[s].append(half[:])
-            elif s < HEAD_STEPS:
+            kind, index = CHUNKS[s]
+            if kind == TAIL_KIND:
+                half = half_pool.tile([P, PACK, BANK], BF16, name="half")
+                nc.sync.dma_start(
+                    out=half[:],
+                    in_=tail_w_0[:, BANK * index : BANK * (index + 1)].rearrange(
+                        "(p t) w -> p t w", t=PACK
+                    ),
+                )
+                raws[s] = [half[:]]
+            elif kind == HEAD_KIND:
                 raw = raw_pool.tile([P, PACK, HEAD], BF16, tag="raw", name="raw")
                 nc.sync.dma_start(
                     out=raw[:],
-                    in_=head_weight[K_PASS * s : K_PASS * (s + 1), :].rearrange(
+                    in_=head_weight[K_PASS * index : K_PASS * (index + 1), :].rearrange(
                         "(p t) w -> p t w", t=PACK
                     ),
                 )
                 raws[s] = [raw[:]]
-            elif s < HEAD_STEPS + PROJ_STEPS:
-                first = 2 * K_PASS * (s - HEAD_STEPS)
-                raw = raw_pool.tile([P, 2, PACK, PROJ], BF16, tag="raw", name="raw")
-                nc.sync.dma_start(
-                    out=raw[:],
-                    in_=tail_proj_0[first : first + 2 * K_PASS, :].rearrange(
-                        "(b p t) w -> p b t w", b=2, t=PACK
-                    ),
-                )
-                raws[s] = [raw[:, b] for b in range(2)]
             else:
-                first = BANK * (s - HEAD_STEPS - PROJ_STEPS)
-                half = half_pool.tile([P, PACK, BANK], BF16, name="half")
-                nc.sync.dma_start(
-                    out=half[:],
-                    in_=tail_w_0[:, first : first + BANK].rearrange("(p t) w -> p t w", t=PACK),
+                rows = tail_proj_0[2 * K_PASS * index : 2 * K_PASS * (index + 1), :].rearrange(
+                    "(b p t) w -> p b t w", b=2, t=PACK
                 )
-                raws[s] = [half[:]]
+                if s == 0:
+                    raws[s] = []
+                    for b in range(2):
+                        half = half_pool.tile([P, PACK, PROJ], BF16, name="half")
+                        nc.sync.dma_start(out=half[:], in_=rows[:, b])
+                        raws[s].append(half[:])
+                else:
+                    raw = raw_pool.tile([P, 2, PACK, PROJ], BF16, tag="raw", name="raw")
+                    nc.sync.dma_start(out=raw[:], in_=rows)
+                    raws[s] = [raw[:, b] for b in range(2)]
 
         def load_x(group):
             columns = slice(X_GROUP * K_PASS * group, X_GROUP * K_PASS * (group + 1))
@@ -121,8 +129,8 @@ def tile_adaptiveinputsoftmax_pa_k_kernel(
             if s >= STEPS:
                 return
             load_weight(s)
-            if s % X_GROUP == 0 and X_DELAY <= s < PASSES + X_DELAY:
-                load_x((s - X_DELAY) // X_GROUP)
+            if s in X_LOAD_STEPS:
+                load_x(X_LOAD_STEPS.index(s))
 
         for s in range(PREFETCH):
             load(s)
@@ -157,7 +165,7 @@ def tile_adaptiveinputsoftmax_pa_k_kernel(
                 raw[:, m, columns].bitcast(F32).rearrange("r (p u) -> r u p", u=2)
                 for m in range(TOKEN_TILES)
             ]
-            x_transposed[c] = bank(4 + c % 2, "xt").rearrange("p (u r) -> p u r", u=2)
+            x_transposed[c] = bank(6, "xt").rearrange("p (u r) -> p u r", u=2)
             transpose_rows(words, x_transposed[c])
 
         def copy_x(c):
@@ -184,12 +192,17 @@ def tile_adaptiveinputsoftmax_pa_k_kernel(
         identity_banks = {}
 
         def shares(s):
-            if s == 0:
-                return [[(VECTOR, 256), (SCALAR, 256)]] * 2
-            if s < HEAD_STEPS:
+            kind, index = CHUNKS[s]
+            if kind == PROJ_KIND:
+                if index == 0:
+                    return [[(VECTOR, 256), (SCALAR, 256)]] * 2
+                if index % 2 == 0:
+                    return [[(VECTOR, 512)], [(SCALAR, 512)]]
+                return [[(VECTOR, 512)], [(SCALAR, 256), (TENSOR, PIECE)]]
+            if kind == HEAD_KIND:
+                if index % 2:
+                    return [[(VECTOR, 448), (SCALAR, 320), (TENSOR, PIECE)]]
                 return [[(VECTOR, 576), (SCALAR, 448)]]
-            if s < HEAD_STEPS + PROJ_STEPS:
-                return [[(VECTOR, 384), (SCALAR, 128)], [(SCALAR, 256), (TENSOR, PIECE)]]
             return [[(VECTOR, 256), (SCALAR, 256)]]
 
         def parts(s, who):
@@ -212,14 +225,14 @@ def tile_adaptiveinputsoftmax_pa_k_kernel(
             return view.rearrange("p t (c i) -> p c t i", i=RUN)
 
         def identity_matmuls(s):
-            for source, target in parts(s, TENSOR):
-                identity_banks[s] = psum.tile(
-                    [P, PIECE, PACK], BF16, tag="bank%d" % (6 + s % 2), name="identity_bank"
+            for number, (source, target) in enumerate(parts(s, TENSOR)):
+                identity_banks[(s, number)] = psum.tile(
+                    [P, PIECE, PACK], BF16, tag="bank%d" % (7 - number), name="identity_bank"
                 )
                 for first in range(0, PIECE, P):
                     columns = slice(first, first + P)
                     nc.tensor.matmul(
-                        out=interleaved(identity_banks[s][:, columns, :]),
+                        out=interleaved(identity_banks[(s, number)][:, columns, :]),
                         lhsT=identity_bf16[:],
                         rhs=by_rows(source[:, :, columns]),
                         start=True,
@@ -231,22 +244,29 @@ def tile_adaptiveinputsoftmax_pa_k_kernel(
                 grouped[s] = grouped_pool.tile(
                     [P, CHUNK, PACK], BF16, align_bytes=64, name="grouped"
                 )
-            for source, columns in parts(s, who):
+            for number, (source, columns) in enumerate(parts(s, who)):
                 target = grouped[s][:, columns, :]
                 if who == VECTOR:
                     nc.vector.tensor_copy(out=interleaved(target), in_=by_rows(source))
                 elif who == SCALAR:
                     nc.scalar.copy(out=interleaved(target), in_=by_rows(source))
                 else:
-                    nc.scalar.copy(out=target, in_=identity_banks[s][:])
+                    nc.scalar.copy(out=target, in_=identity_banks[(s, number)][:])
 
         codes = {}
+        tail_codes = keep.tile([P, TAIL], U32, align_bytes=64, name="tail_codes")
+        tail_scales = keep.tile([P, TAIL], U8, align_bytes=64, name="tail_scales")
 
         def quantise(s):
             width = sum(columns for block in shares(s) for engine, columns in block)
-            code = codes_pool.tile([P, CHUNK], U32, align_bytes=64, name="code")
-            scale = codes_pool.tile([P, CHUNK], U8, align_bytes=64, name="scale")
-            codes[s] = (code[:, 0:width], scale[:, 0:width])
+            kind, index = CHUNKS[s]
+            if kind == TAIL_KIND:
+                columns = slice(BANK * index, BANK * (index + 1))
+                codes[s] = (tail_codes[:, columns], tail_scales[:, columns])
+            else:
+                code = codes_pool.tile([P, CHUNK], U32, align_bytes=64, name="code")
+                scale = codes_pool.tile([P, CHUNK], U8, align_bytes=64, name="scale")
+                codes[s] = (code[:], scale[:])
             nc.vector.quantize_mx(
                 out=codes[s][0].bitcast(FP8X4),
                 scales=codes[s][1],
@@ -264,47 +284,43 @@ def tile_adaptiveinputsoftmax_pa_k_kernel(
                 stop=stop,
             )
 
-        head_acc = []
-        h_acc = []
+        head_acc = [
+            [bank(HEAD_BANKS * m + n, "head_acc") for n in range(HEAD_BANKS)]
+            for m in range(TOKEN_TILES)
+        ]
+        h_acc = [bank(4 + m, "h_acc") for m in range(TOKEN_TILES)]
         tail_logits = {}
-        TAIL_BANK_ORDER = (0, 1, 2, 6, 7, 4, 5, 3)
+        TAIL_BANK_ORDER = ((4, 5, 7, 6), (0, 1, 2, 3))
 
         def x_tokens(c, m):
             return slice(TOKENS * c + P * m, TOKENS * c + P * (m + 1))
 
         def multiply(s):
-            if s == 0:
-                for m in range(TOKEN_TILES):
-                    head_acc.append(
-                        [bank(HEAD_BANKS * m + n, "head_acc") for n in range(HEAD_BANKS)]
-                    )
-            if s < HEAD_STEPS:
-                for m in range(TOKEN_TILES):
+            kind, index = CHUNKS[s]
+            for m in range(TOKEN_TILES):
+                if kind == HEAD_KIND:
                     for n in range(HEAD_BANKS):
                         multiply_pass(
-                            head_acc[m][n], (x_codes, x_scales), x_tokens(s, m),
+                            head_acc[m][n], (x_codes, x_scales), x_tokens(index, m),
                             codes[s], slice(BANK * n, BANK * (n + 1)),
-                            s == 0, s == PASSES - 1,
+                            index == 0, index == PASSES - 1,
                         )
-            elif s < HEAD_STEPS + PROJ_STEPS:
-                if s == HEAD_STEPS:
-                    h_acc.extend([bank(4 + m, "h_acc") for m in range(TOKEN_TILES)])
-                for b in range(2):
-                    c = 2 * (s - HEAD_STEPS) + b
-                    for m in range(TOKEN_TILES):
+                else:
+                    for b in range(2):
+                        c = 2 * index + b
                         multiply_pass(
                             h_acc[m], (x_codes, x_scales), x_tokens(c, m),
                             codes[s], slice(BANK * b, BANK * (b + 1)),
                             c == 0, c == PASSES - 1,
                         )
-            else:
-                n = s - HEAD_STEPS - PROJ_STEPS
-                for m in range(TOKEN_TILES):
-                    tail_logits[(m, n)] = bank(TAIL_BANK_ORDER[TOKEN_TILES * n + m], "tail_logits")
-                    multiply_pass(
-                        tail_logits[(m, n)], (h_codes, h_scales), slice(P * m, P * (m + 1)),
-                        codes[s], slice(0, BANK), True, True,
-                    )
+
+        def multiply_tail(n, m):
+            columns = slice(BANK * n, BANK * (n + 1))
+            tail_logits[(n, m)] = bank(TAIL_BANK_ORDER[m][n], "tail_logits")
+            multiply_pass(
+                tail_logits[(n, m)], (h_codes, h_scales), slice(P * m, P * (m + 1)),
+                (tail_codes, tail_scales), columns, True, True,
+            )
 
         head_exp = stats("head_exp", HEAD)
         head_bank_max = stats("head_bank_max", HEAD_BANKS)
@@ -341,19 +357,23 @@ def tile_adaptiveinputsoftmax_pa_k_kernel(
         def invert_head(m):
             nc.vector.reciprocal(out=head_inverse[m][:], in_=head_sum[m][:])
 
-        def scale_head(m):
-            for source, target in (
-                (slice(HEAD_TOKENS, HEAD_TOKENS + 1), cluster0[m][:]),
-                (slice(HEAD_TOKENS + 1, HEAD_TOKENS + 2), cluster1[:, m : m + 1]),
-                (slice(0, HEAD_TOKENS), head_exp[m][:, 0:HEAD_TOKENS]),
-            ):
+        def scale_clusters(m):
+            for column, target in ((0, cluster0[m][:]), (1, cluster1[:, m : m + 1])):
                 nc.vector.tensor_scalar(
                     out=target,
-                    in0=head_exp[m][:, source],
+                    in0=head_exp[m][:, HEAD_TOKENS + column : HEAD_TOKENS + column + 1],
                     scalar1=head_inverse[m][:],
                     scalar2=None,
                     op0=MULT,
                 )
+
+        def scale_head(m):
+            nc.scalar.activation(
+                out=head_exp[m][:, 0:HEAD_TOKENS],
+                in_=head_exp[m][:, 0:HEAD_TOKENS],
+                func=COPY,
+                scale=head_inverse[m][:],
+            )
 
         def store_head(m):
             nc.sync.dma_start(out=out_0[m, :, 0:HEAD_TOKENS], in_=head_exp[m][:, 0:HEAD_TOKENS])
@@ -362,7 +382,7 @@ def tile_adaptiveinputsoftmax_pa_k_kernel(
         cluster1_out = keep.tile([P, P], F32, name="cluster1_out")
 
         def turn_cluster1():
-            rows = bank(2, "cluster1_rows")
+            rows = bank(4, "cluster1_rows")
             nc.tensor.transpose(rows[:, 0:P], cluster1[:], identity[:])
             cluster1_rows.append(rows)
 
@@ -381,11 +401,11 @@ def tile_adaptiveinputsoftmax_pa_k_kernel(
         h_transposed = []
 
         def round_h():
-            nc.vector.tensor_copy(out=h_rounded[0][:], in_=h_acc[0])
-            nc.scalar.copy(out=h_rounded[1][:], in_=h_acc[1])
+            for m in range(TOKEN_TILES):
+                nc.scalar.copy(out=h_rounded[m][:], in_=h_acc[m])
 
         def transpose_h():
-            h_transposed.append(bank(3, "ht").rearrange("p (u r) -> p u r", u=2))
+            h_transposed.append(bank(6, "ht").rearrange("p (u r) -> p u r", u=2))
             words = [
                 h_rounded[m][:].bitcast(F32).rearrange("r (p u) -> r u p", u=2)
                 for m in range(TOKEN_TILES)
@@ -418,7 +438,7 @@ def tile_adaptiveinputsoftmax_pa_k_kernel(
         def max_bank(n, m):
             nc.vector.tensor_reduce(
                 out=bank_neg_max[m][:, n : n + 1],
-                in_=tail_logits[(m, n)],
+                in_=tail_logits[(n, m)],
                 axis=ALONG_ROW,
                 op=MAX,
                 negate=True,
@@ -427,7 +447,7 @@ def tile_adaptiveinputsoftmax_pa_k_kernel(
         def exp_bank(n, m):
             nc.scalar.activation(
                 out=tail_exp[m][:, BANK * n : BANK * (n + 1)],
-                in_=tail_logits[(m, n)],
+                in_=tail_logits[(n, m)],
                 func=EXP,
                 bias=bank_neg_max[m][:, n : n + 1],
                 accum_out=bank_sum[m][:, n : n + 1],
@@ -460,7 +480,7 @@ def tile_adaptiveinputsoftmax_pa_k_kernel(
         def add_sums(m):
             nc.vector.reduce_sum(out=early_sum[m][:], in_=scaled_sum[m][:], axis=ALONG_ROW)
 
-        def invert_sum(m):
+        def join_sums(m):
             nc.vector.scalar_tensor_tensor(
                 out=tail_sum[m][:],
                 in0=bank_sum[m][:, LAST:TAIL_BANKS],
@@ -469,123 +489,120 @@ def tile_adaptiveinputsoftmax_pa_k_kernel(
                 op0=MULT,
                 op1=ADD,
             )
+
+        def invert_tail(m):
             nc.vector.reciprocal(out=tail_inverse[m][:], in_=tail_sum[m][:])
 
-        def store_tail(m):
-            for n in range(TAIL_BANKS):
-                columns = slice(BANK * n, BANK * (n + 1))
-                nc.vector.tensor_scalar(
-                    out=tail_exp[m][:, columns],
-                    in0=tail_exp[m][:, columns],
-                    scalar1=cluster_factor[m][:, n : n + 1],
-                    scalar2=tail_inverse[m][:],
-                    op0=MULT,
-                    op1=MULT,
-                )
-                nc.sync.dma_start(
-                    out=out_0[m, :, HEAD_TOKENS + BANK * n : HEAD_TOKENS + BANK * (n + 1)],
-                    in_=tail_exp[m][:, columns],
-                )
+        def scale_bank(n, m):
+            columns = slice(BANK * n, BANK * (n + 1))
+            nc.vector.tensor_scalar(
+                out=tail_exp[m][:, columns],
+                in0=tail_exp[m][:, columns],
+                scalar1=cluster_factor[m][:, n : n + 1],
+                scalar2=tail_inverse[m][:],
+                op0=MULT,
+                op1=MULT,
+            )
+            nc.sync.dma_start(
+                out=out_0[m, :, HEAD_TOKENS + BANK * n : HEAD_TOKENS + BANK * (n + 1)],
+                in_=tail_exp[m][:, columns],
+            )
 
-        first_tail = HEAD_STEPS + PROJ_STEPS
-        quantised_in = {1: [0], 2: [1]}
-        for s in range(4, first_tail - 1):
-            quantised_in[s] = [s - 2]
-        quantised_in[first_tail - 1] = [first_tail - 3, first_tail - 2]
-        for s in range(first_tail, STEPS):
-            quantised_in[s] = [s - 1]
-        multiplied_in = {s: [s - 5] for s in range(5, HEAD_STEPS + 3)}
-        for i in range(2):
-            multiplied_in[HEAD_STEPS + 3 + i] = [HEAD_STEPS - 2 + 2 * i, HEAD_STEPS - 1 + 2 * i]
-        for s in range(HEAD_STEPS + 5, first_tail):
-            multiplied_in[s] = [s - 3]
-        multiplied_in[first_tail] = [first_tail - 3, first_tail - 2, first_tail - 1]
-        softmax_step = HEAD_STEPS + 4
-        before_regrouping = {
-            softmax_step + 1: lambda: join_head_max(0),
-            softmax_step + 2: lambda: join_head_max(1),
-            softmax_step + 3: lambda: scale_head(0),
-            softmax_step + 4: lambda: scale_head(1),
+        x_transposed_in = {
+            s + 1 + i: [X_GROUP * g + i] for g, s in enumerate(PROJ_STEPS) for i in range(X_GROUP)
         }
-        after_regrouping = {
-            softmax_step + 2: lambda: sum_head(0),
-            softmax_step + 3: lambda: sum_head(1),
-            first_tail + 3: quantise_h,
-        }
-        after_quantising = {
-            softmax_step: lambda: max_head(0),
-            softmax_step + 1: lambda: max_head(1),
-            softmax_step + 2: lambda: invert_head(0),
-            softmax_step + 3: lambda: invert_head(1),
-        }
+        x_transposed_in[PROJ_STEPS[0] + 1] = [0, 1]
+        x_quantised_in = {s + 1 + X_GROUP: g for g, s in enumerate(PROJ_STEPS)}
+        x_quantised_in[PROJ_STEPS[0] + 2] = 0
+        multiplied_in = {s: [s - 4] for s in range(4, FIRST_TAIL - 1)}
+        multiplied_in[FIRST_TAIL - 1] = [FIRST_TAIL - 5, FIRST_TAIL - 4]
+        multiplied_in[FIRST_TAIL] = [FIRST_TAIL - 3, FIRST_TAIL - 2]
+        multiplied_in[FIRST_TAIL + 1] = [FIRST_TAIL - 1]
 
         identity_matmuls(0)
         for s in range(STEPS):
             load(s + PREFETCH)
-            if s in (softmax_step + 4, softmax_step + 5):
-                store_head(s - softmax_step - 4)
-            if s == STEPS - 1:
-                store_cluster1()
-            x_pass = s - X_DELAY
-            if 0 <= x_pass < PASSES:
-                transpose_x(x_pass)
-            if s + 1 < STEPS:
-                identity_matmuls(s + 1)
-            regroup(s, SCALAR)
-            if 0 <= x_pass < PASSES:
-                copy_x(x_pass)
-            regroup(s, TENSOR)
-            if s <= X_DELAY:
-                for job in quantised_in.get(s, []):
-                    quantise(job)
-            if s in before_regrouping:
-                before_regrouping[s]()
-            regroup(s, VECTOR)
-            if x_pass % X_GROUP == 0 and X_GROUP <= x_pass <= PASSES:
-                quantise_x(x_pass // X_GROUP - 1)
-            if s in after_regrouping:
-                after_regrouping[s]()
-            if s > X_DELAY:
-                for job in quantised_in.get(s, []):
-                    quantise(job)
-            if s in after_quantising:
-                after_quantising[s]()
-            if s in (softmax_step + 1, softmax_step + 2):
-                exp_head(s - softmax_step - 1)
-            for job in multiplied_in.get(s, []):
-                multiply(job)
-            if s == first_tail + 1:
+            if s == FIRST_TAIL:
                 round_h()
                 transpose_h()
-                turn_cluster1()
-            if s == first_tail + 2:
+            regroup(s, SCALAR)
+            for c in x_transposed_in.get(s, []):
+                transpose_x(c)
+                copy_x(c)
+            regroup(s, TENSOR)
+            if s == FIRST_TAIL:
                 copy_h()
-                copy_cluster1()
-        for n in range(TAIL_BANKS):
-            if n == 1:
-                quantise(first_tail + LAST)
-            multiply(first_tail + n)
-            max_bank(n, 0)
-            exp_bank(n, 0)
-        max_bank(0, 1)
+            regroup(s, VECTOR)
+            if s == FIRST_TAIL + 1:
+                quantise_h()
+            if s in x_quantised_in:
+                quantise_x(x_quantised_in[s])
+            if s > 0:
+                quantise(s - 1)
+            for job in multiplied_in.get(s, []):
+                multiply(job)
+            if s + 1 < STEPS:
+                identity_matmuls(s + 1)
+            if s == STEPS - 2:
+                multiply_tail(0, 0)
+                max_head(0)
+            if s == STEPS - 1:
+                join_head_max(0)
+                exp_head(0)
+                max_head(1)
+        quantise(STEPS - 1)
+        join_head_max(1)
+        exp_head(1)
+        for n in range(1, TAIL_BANKS):
+            multiply_tail(n, 0)
+        max_bank(0, 0)
+        exp_bank(0, 0)
+        sum_head(0)
+        max_bank(1, 0)
+        exp_bank(1, 0)
+        invert_head(0)
+        sum_head(1)
+        max_bank(2, 0)
+        exp_bank(2, 0)
+        invert_head(1)
+        scale_clusters(0)
+        max_bank(3, 0)
+        exp_bank(3, 0)
+        scale_clusters(1)
         join_tail_max(0)
+        scale_head(0)
+        store_head(0)
         exp_factor(0)
+        for n in range(TAIL_BANKS):
+            multiply_tail(n, 1)
+        max_bank(0, 1)
         exp_bank(0, 1)
         max_bank(1, 1)
-        exp_bank(1, 1)
         scale_factor(0)
         scale_sums(0)
+        scale_head(1)
+        store_head(1)
+        exp_bank(1, 1)
+        add_sums(0)
+        turn_cluster1()
         max_bank(2, 1)
         exp_bank(2, 1)
-        add_sums(0)
+        join_sums(0)
         max_bank(3, 1)
-        invert_sum(0)
+        invert_tail(0)
         join_tail_max(1)
         exp_factor(1)
         exp_bank(3, 1)
-        store_tail(0)
+        copy_cluster1()
+        scale_bank(0, 0)
+        scale_bank(1, 0)
         scale_factor(1)
         scale_sums(1)
+        scale_bank(2, 0)
         add_sums(1)
-        invert_sum(1)
-        store_tail(1)
+        scale_bank(3, 0)
+        join_sums(1)
+        invert_tail(1)
+        for n in range(TAIL_BANKS):
+            scale_bank(n, 1)
+        store_cluster1()

@@ -54,8 +54,9 @@ CHUNKS = (
 STEPS = len(CHUNKS)
 FIRST_TAIL = STEPS - TAIL_BANKS
 PROJ_STEPS = [s for s in range(STEPS) if CHUNKS[s][0] == PROJ_KIND]
-X_LOAD_STEPS = [PROJ_STEPS[0] + 1, PROJ_STEPS[1] + 1] + PROJ_STEPS[2:]
+X_LOAD_STEPS = [PROJ_STEPS[0] + 2, PROJ_STEPS[1] + 2] + PROJ_STEPS[2:]
 PREFETCH = 6
+EARLY_STEPS = 3
 
 FLOPS = 2 * TOKENS * D * (HEAD + PROJ) + 2 * TOKENS * PROJ * TAIL
 
@@ -77,6 +78,12 @@ def tile_adaptiveinputsoftmax_pa_k_kernel(
 
         def bank(index, name):
             return psum.tile([P, BANK], F32, tag="bank%d" % index, name=name)[:]
+
+        scratch_banks = []
+
+        def scratch_bank():
+            scratch_banks.append(6 + len(scratch_banks) % 2)
+            return scratch_banks[-1]
 
         def stats(name, width):
             return [keep.tile([P, width], F32, name=name + str(m)) for m in range(TOKEN_TILES)]
@@ -165,7 +172,7 @@ def tile_adaptiveinputsoftmax_pa_k_kernel(
                 raw[:, m, columns].bitcast(F32).rearrange("r (p u) -> r u p", u=2)
                 for m in range(TOKEN_TILES)
             ]
-            x_transposed[c] = bank(6, "xt").rearrange("p (u r) -> p u r", u=2)
+            x_transposed[c] = bank(scratch_bank(), "xt").rearrange("p (u r) -> p u r", u=2)
             transpose_rows(words, x_transposed[c])
 
         def copy_x(c):
@@ -227,7 +234,7 @@ def tile_adaptiveinputsoftmax_pa_k_kernel(
         def identity_matmuls(s):
             for number, (source, target) in enumerate(parts(s, TENSOR)):
                 identity_banks[(s, number)] = psum.tile(
-                    [P, PIECE, PACK], BF16, tag="bank%d" % (7 - number), name="identity_bank"
+                    [P, PIECE, PACK], BF16, tag="bank%d" % scratch_bank(), name="identity_bank"
                 )
                 for first in range(0, PIECE, P):
                     columns = slice(first, first + P)
@@ -511,9 +518,10 @@ def tile_adaptiveinputsoftmax_pa_k_kernel(
         x_transposed_in = {
             s + 1 + i: [X_GROUP * g + i] for g, s in enumerate(PROJ_STEPS) for i in range(X_GROUP)
         }
-        x_transposed_in[PROJ_STEPS[0] + 1] = [0, 1]
+        x_transposed_in[PROJ_STEPS[0] + 1] = []
+        x_transposed_in[PROJ_STEPS[0] + 2] = [0, 1]
+        x_transposed_in[PROJ_STEPS[1] + 2] = [2, 3]
         x_quantised_in = {s + 1 + X_GROUP: g for g, s in enumerate(PROJ_STEPS)}
-        x_quantised_in[PROJ_STEPS[0] + 2] = 0
         multiplied_in = {s: [s - 4] for s in range(4, FIRST_TAIL - 1)}
         multiplied_in[FIRST_TAIL - 1] = [FIRST_TAIL - 5, FIRST_TAIL - 4]
         multiplied_in[FIRST_TAIL] = [FIRST_TAIL - 3, FIRST_TAIL - 2]
@@ -526,18 +534,20 @@ def tile_adaptiveinputsoftmax_pa_k_kernel(
                 round_h()
                 transpose_h()
             regroup(s, SCALAR)
+            regroup(s, TENSOR)
             for c in x_transposed_in.get(s, []):
                 transpose_x(c)
                 copy_x(c)
-            regroup(s, TENSOR)
             if s == FIRST_TAIL:
                 copy_h()
+            if 0 < s < EARLY_STEPS:
+                quantise(s - 1)
             regroup(s, VECTOR)
             if s == FIRST_TAIL + 1:
                 quantise_h()
             if s in x_quantised_in:
                 quantise_x(x_quantised_in[s])
-            if s > 0:
+            if s >= EARLY_STEPS:
                 quantise(s - 1)
             for job in multiplied_in.get(s, []):
                 multiply(job)
@@ -570,16 +580,16 @@ def tile_adaptiveinputsoftmax_pa_k_kernel(
         exp_bank(3, 0)
         scale_clusters(1)
         join_tail_max(0)
+        exp_factor(0)
         scale_head(0)
         store_head(0)
-        exp_factor(0)
         for n in range(TAIL_BANKS):
             multiply_tail(n, 1)
         max_bank(0, 1)
-        exp_bank(0, 1)
-        max_bank(1, 1)
         scale_factor(0)
+        exp_bank(0, 1)
         scale_sums(0)
+        max_bank(1, 1)
         scale_head(1)
         store_head(1)
         exp_bank(1, 1)

@@ -9,7 +9,6 @@ U32 = mybir.dt.uint32
 U8 = mybir.dt.uint8
 FP8X4 = mybir.dt.float8_e4m3fn_x4
 EXP = mybir.ActivationFunctionType.Exp
-COPY = mybir.ActivationFunctionType.Copy
 MULT = mybir.AluOpType.mult
 MAX = mybir.AluOpType.max
 MIN = mybir.AluOpType.min
@@ -366,20 +365,23 @@ def tile_adaptiveinputsoftmax_pa_k_kernel(
 
         def scale_clusters(m):
             for column, target in ((0, cluster0[m][:]), (1, cluster1[:, m : m + 1])):
-                nc.vector.tensor_scalar(
+                nc.gpsimd.tensor_scalar(
                     out=target,
                     in0=head_exp[m][:, HEAD_TOKENS + column : HEAD_TOKENS + column + 1],
                     scalar1=head_inverse[m][:],
-                    scalar2=None,
+                    scalar2=0.0,
                     op0=MULT,
+                    op1=ADD,
                 )
 
         def scale_head(m):
-            nc.scalar.activation(
+            nc.gpsimd.tensor_scalar(
                 out=head_exp[m][:, 0:HEAD_TOKENS],
-                in_=head_exp[m][:, 0:HEAD_TOKENS],
-                func=COPY,
-                scale=head_inverse[m][:],
+                in0=head_exp[m][:, 0:HEAD_TOKENS],
+                scalar1=head_inverse[m][:],
+                scalar2=0.0,
+                op0=MULT,
+                op1=ADD,
             )
 
         def store_head(m):
@@ -576,41 +578,41 @@ def tile_adaptiveinputsoftmax_pa_k_kernel(
         exp_bank(2, 0)
         invert_head(1)
         scale_clusters(0)
+        scale_head(0)
+        store_head(0)
         max_bank(3, 0)
         exp_bank(3, 0)
         scale_clusters(1)
+        scale_head(1)
+        store_head(1)
         join_tail_max(0)
         exp_factor(0)
-        scale_head(0)
-        store_head(0)
         for n in range(TAIL_BANKS):
             multiply_tail(n, 1)
         max_bank(0, 1)
+        scale_sums(0)
         scale_factor(0)
         exp_bank(0, 1)
-        scale_sums(0)
-        max_bank(1, 1)
-        scale_head(1)
-        store_head(1)
-        exp_bank(1, 1)
         add_sums(0)
+        max_bank(1, 1)
+        exp_bank(1, 1)
+        join_sums(0)
         turn_cluster1()
         max_bank(2, 1)
         exp_bank(2, 1)
-        join_sums(0)
-        max_bank(3, 1)
         invert_tail(0)
+        max_bank(3, 1)
+        scale_bank(0, 0)
         join_tail_max(1)
         exp_factor(1)
         exp_bank(3, 1)
         copy_cluster1()
-        scale_bank(0, 0)
         scale_bank(1, 0)
-        scale_factor(1)
-        scale_sums(1)
         scale_bank(2, 0)
-        add_sums(1)
+        scale_sums(1)
+        scale_factor(1)
         scale_bank(3, 0)
+        add_sums(1)
         join_sums(1)
         invert_tail(1)
         for n in range(TAIL_BANKS):

@@ -206,9 +206,7 @@ def tile_adaptiveinputsoftmax_pa_k_kernel(
                     return [[(VECTOR, 512)], [(SCALAR, 512)]]
                 return [[(VECTOR, 512)], [(SCALAR, 256), (TENSOR, PIECE)]]
             if kind == HEAD_KIND:
-                if index % 2:
-                    return [[(VECTOR, 448), (SCALAR, 320), (TENSOR, PIECE)]]
-                return [[(VECTOR, 576), (SCALAR, 448)]]
+                return [[(VECTOR, 544), (SCALAR, 480)]]
             return [[(VECTOR, 256), (SCALAR, 256)]]
 
         def parts(s, who):

from contextlib import ExitStack

import concourse.mybir as mybir
from concourse.masks import make_identity

F32 = mybir.dt.float32
BF16 = mybir.dt.bfloat16
U32 = mybir.dt.uint32
U8 = mybir.dt.uint8
FP8X4 = mybir.dt.float8_e4m3fn_x4
EXP = mybir.ActivationFunctionType.Exp
MULT = mybir.AluOpType.mult
MAX = mybir.AluOpType.max
MIN = mybir.AluOpType.min
ADD = mybir.AluOpType.add
ALONG_ROW = mybir.AxisListType.X

P = 128
PACK = 4
K_PASS = P * PACK
BANK = 512

TOKEN_TILES = 2
TOKENS = TOKEN_TILES * P
D = 8192
PASSES = D // K_PASS
HEAD = 1024
HEAD_TOKENS = 1022
HEAD_BANKS = HEAD // BANK
PROJ = 512
TAIL = 2048
TAIL_BANKS = TAIL // BANK

CHUNK = 2 * BANK
X_GROUP = 2
RUN = 4
PIECE = 256
VECTOR, SCALAR, TENSOR = 0, 1, 2

GROUPS = PASSES // X_GROUP
PROJ_KIND, HEAD_KIND, TAIL_KIND = 0, 1, 2

CHUNKS = (
    [(PROJ_KIND, 0)]
    + [
        chunk
        for g in range(1, GROUPS)
        for chunk in ((PROJ_KIND, g), (HEAD_KIND, 2 * g - 2), (HEAD_KIND, 2 * g - 1))
    ]
    + [(HEAD_KIND, PASSES - 2), (HEAD_KIND, PASSES - 1)]
    + [(TAIL_KIND, n) for n in range(TAIL_BANKS)]
)
STEPS = len(CHUNKS)
FIRST_TAIL = STEPS - TAIL_BANKS
PROJ_STEPS = [s for s in range(STEPS) if CHUNKS[s][0] == PROJ_KIND]
X_LOAD_STEPS = [PROJ_STEPS[0] + 2, PROJ_STEPS[1] + 2] + PROJ_STEPS[2:]
PREFETCH = 6
EARLY_STEPS = 3

FLOPS = 2 * TOKENS * D * (HEAD + PROJ) + 2 * TOKENS * PROJ * TAIL


def tile_adaptiveinputsoftmax_pa_k_kernel(
    tc, x, head_weight, tail_proj_0, tail_w_0, out_0, out_1
):
    nc = tc.nc
    with ExitStack() as ctx:
        keep = ctx.enter_context(tc.tile_pool(name="keep", bufs=1))
        x_pool = ctx.enter_context(tc.tile_pool(name="x_pool", bufs=5))
        x_grouped_pool = ctx.enter_context(tc.tile_pool(name="x_grouped_pool", bufs=3))
        raw_pool = ctx.enter_context(tc.tile_pool(name="raw_pool", bufs=PREFETCH + 1))
        half_pool = ctx.enter_context(tc.tile_pool(name="half_pool", bufs=TAIL_BANKS))
        grouped_pool = ctx.enter_context(tc.tile_pool(name="grouped_pool", bufs=4))
        codes_pool = ctx.enter_context(tc.tile_pool(name="codes_pool", bufs=6))
        psum = ctx.enter_context(tc.psum_pool(name="psum", bufs=1))
        ctx.enter_context(tc.manual_schedule())

        def bank(index, name):
            return psum.tile([P, BANK], F32, tag="bank%d" % index, name=name)[:]

        scratch_banks = []

        def scratch_bank():
            scratch_banks.append(6 + len(scratch_banks) % 2)
            return scratch_banks[-1]

        def stats(name, width):
            return [keep.tile([P, width], F32, name=name + str(m)) for m in range(TOKEN_TILES)]

        raws = {}
        x_raws = {}

        def load_weight(s):
            kind, index = CHUNKS[s]
            if kind == TAIL_KIND:
                half = half_pool.tile([P, PACK, BANK], BF16, name="half")
                nc.sync.dma_start(
                    out=half[:],
                    in_=tail_w_0[:, BANK * index : BANK * (index + 1)].rearrange(
                        "(p t) w -> p t w", t=PACK
                    ),
                )
                raws[s] = [half[:]]
            elif kind == HEAD_KIND:
                raw = raw_pool.tile([P, PACK, HEAD], BF16, tag="raw", name="raw")
                nc.sync.dma_start(
                    out=raw[:],
                    in_=head_weight[K_PASS * index : K_PASS * (index + 1), :].rearrange(
                        "(p t) w -> p t w", t=PACK
                    ),
                )
                raws[s] = [raw[:]]
            else:
                rows = tail_proj_0[2 * K_PASS * index : 2 * K_PASS * (index + 1), :].rearrange(
                    "(b p t) w -> p b t w", b=2, t=PACK
                )
                if s == 0:
                    raws[s] = []
                    for b in range(2):
                        half = half_pool.tile([P, PACK, PROJ], BF16, name="half")
                        nc.sync.dma_start(out=half[:], in_=rows[:, b])
                        raws[s].append(half[:])
                else:
                    raw = raw_pool.tile([P, 2, PACK, PROJ], BF16, tag="raw", name="raw")
                    nc.sync.dma_start(out=raw[:], in_=rows)
                    raws[s] = [raw[:, b] for b in range(2)]

        def load_x(group):
            columns = slice(X_GROUP * K_PASS * group, X_GROUP * K_PASS * (group + 1))
            raw = x_pool.tile([P, TOKEN_TILES, X_GROUP * K_PASS], BF16, name="x_raw")
            nc.sync.dma_start(out=raw[:], in_=x[:, :, columns].rearrange("m r k -> r m k"))
            x_raws[group] = raw

        def load(s):
            if s >= STEPS:
                return
            load_weight(s)
            if s in X_LOAD_STEPS:
                load_x(X_LOAD_STEPS.index(s))

        for s in range(PREFETCH):
            load(s)

        zero = keep.tile([P, 1], F32, name="zero")
        one = keep.tile([P, 1], F32, name="one")
        nc.vector.memset(zero[:], 0.0)
        nc.scalar.activation(out=one[:], in_=zero[:], func=EXP)
        identity = keep.tile([P, P], F32, name="identity")
        make_identity(nc, identity[:])
        identity_bf16 = keep.tile([P, P], BF16, name="identity_bf16")
        make_identity(nc, identity_bf16[:])
        cluster1 = keep.tile([P, P], F32, name="cluster1")
        nc.vector.memset(cluster1[:], 0.0)

        x_codes = keep.tile([P, PASSES * TOKENS], U32, align_bytes=64, name="x_codes")
        x_scales = keep.tile([P, PASSES * TOKENS], U8, align_bytes=64, name="x_scales")
        x_transposed = {}
        x_grouped = {}

        def transpose_rows(words, target):
            for u in range(2):
                for m in range(TOKEN_TILES):
                    nc.tensor.transpose(
                        target[:, u, P * m : P * (m + 1)], words[m][:, u, :], identity[:]
                    )

        def transpose_x(c):
            raw = x_raws[c // X_GROUP]
            columns = slice(K_PASS * (c % X_GROUP), K_PASS * (c % X_GROUP + 1))
            words = [
                raw[:, m, columns].bitcast(F32).rearrange("r (p u) -> r u p", u=2)
                for m in range(TOKEN_TILES)
            ]
            x_transposed[c] = bank(scratch_bank(), "xt").rearrange("p (u r) -> p u r", u=2)
            transpose_rows(words, x_transposed[c])

        def copy_x(c):
            if c % X_GROUP == 0:
                x_grouped[c // X_GROUP] = x_grouped_pool.tile(
                    [P, X_GROUP * TOKENS * PACK], BF16, align_bytes=64, name="x_grouped"
                )
            words = x_grouped[c // X_GROUP][:].bitcast(F32).rearrange(
                "p (g r u) -> p g r u", g=X_GROUP, u=2
            )
            nc.scalar.copy(
                out=words[:, c % X_GROUP], in_=x_transposed[c].rearrange("p u r -> p r u")
            )

        def quantise_x(group):
            columns = slice(X_GROUP * TOKENS * group, X_GROUP * TOKENS * (group + 1))
            nc.vector.quantize_mx(
                out=x_codes[:, columns].bitcast(FP8X4),
                scales=x_scales[:, columns],
                in_=x_grouped[group][:],
            )

        grouped = {}
        identity_banks = {}

        def shares(s):
            kind, index = CHUNKS[s]
            if kind == PROJ_KIND:
                if index == 0:
                    return [[(VECTOR, 256), (SCALAR, 256)]] * 2
                if index % 2 == 0:
                    return [[(VECTOR, 512)], [(SCALAR, 512)]]
                return [[(VECTOR, 512)], [(SCALAR, 256), (TENSOR, PIECE)]]
            if kind == HEAD_KIND:
                return [[(VECTOR, 544), (SCALAR, 480)]]
            return [[(VECTOR, 256), (SCALAR, 256)]]

        def parts(s, who):
            found = []
            width = 0
            for raw, block in zip(raws[s], shares(s)):
                first = 0
                for engine, columns in block:
                    if engine == who:
                        source = raw[:, :, first : first + columns]
                        found.append((source, slice(width, width + columns)))
                    first += columns
                    width += columns
            return found

        def interleaved(view):
            return view.rearrange("p (c i) t -> p c t i", i=RUN)

        def by_rows(view):
            return view.rearrange("p t (c i) -> p c t i", i=RUN)

        def identity_matmuls(s):
            for number, (source, target) in enumerate(parts(s, TENSOR)):
                identity_banks[(s, number)] = psum.tile(
                    [P, PIECE, PACK], BF16, tag="bank%d" % scratch_bank(), name="identity_bank"
                )
                for first in range(0, PIECE, P):
                    columns = slice(first, first + P)
                    nc.tensor.matmul(
                        out=interleaved(identity_banks[(s, number)][:, columns, :]),
                        lhsT=identity_bf16[:],
                        rhs=by_rows(source[:, :, columns]),
                        start=True,
                        stop=True,
                    )

        def regroup(s, who):
            if s not in grouped:
                grouped[s] = grouped_pool.tile(
                    [P, CHUNK, PACK], BF16, align_bytes=64, name="grouped"
                )
            for number, (source, columns) in enumerate(parts(s, who)):
                target = grouped[s][:, columns, :]
                if who == VECTOR:
                    nc.vector.tensor_copy(out=interleaved(target), in_=by_rows(source))
                elif who == SCALAR:
                    nc.scalar.copy(out=interleaved(target), in_=by_rows(source))
                else:
                    nc.scalar.copy(out=target, in_=identity_banks[(s, number)][:])

        codes = {}
        tail_codes = keep.tile([P, TAIL], U32, align_bytes=64, name="tail_codes")
        tail_scales = keep.tile([P, TAIL], U8, align_bytes=64, name="tail_scales")

        def quantise(s):
            width = sum(columns for block in shares(s) for engine, columns in block)
            kind, index = CHUNKS[s]
            if kind == TAIL_KIND:
                columns = slice(BANK * index, BANK * (index + 1))
                codes[s] = (tail_codes[:, columns], tail_scales[:, columns])
            else:
                code = codes_pool.tile([P, CHUNK], U32, align_bytes=64, name="code")
                scale = codes_pool.tile([P, CHUNK], U8, align_bytes=64, name="scale")
                codes[s] = (code[:], scale[:])
            nc.vector.quantize_mx(
                out=codes[s][0].bitcast(FP8X4),
                scales=codes[s][1],
                in_=grouped[s][:, 0:width, :].rearrange("p w t -> p (w t)"),
            )

        def multiply_pass(out, left, left_columns, right, right_columns, start, stop):
            nc.tensor.matmul_mx(
                out=out,
                lhsT=left[0][:, left_columns].bitcast(FP8X4),
                lhsT_scale=left[1][:, left_columns],
                rhs=right[0][:, right_columns].bitcast(FP8X4),
                rhs_scale=right[1][:, right_columns],
                start=start,
                stop=stop,
            )

        head_acc = [
            [bank(HEAD_BANKS * m + n, "head_acc") for n in range(HEAD_BANKS)]
            for m in range(TOKEN_TILES)
        ]
        h_acc = [bank(4 + m, "h_acc") for m in range(TOKEN_TILES)]
        tail_logits = {}
        TAIL_BANK_ORDER = ((4, 5, 7, 6), (0, 1, 2, 3))

        def x_tokens(c, m):
            return slice(TOKENS * c + P * m, TOKENS * c + P * (m + 1))

        def multiply(s):
            kind, index = CHUNKS[s]
            for m in range(TOKEN_TILES):
                if kind == HEAD_KIND:
                    for n in range(HEAD_BANKS):
                        multiply_pass(
                            head_acc[m][n], (x_codes, x_scales), x_tokens(index, m),
                            codes[s], slice(BANK * n, BANK * (n + 1)),
                            index == 0, index == PASSES - 1,
                        )
                else:
                    for b in range(2):
                        c = 2 * index + b
                        multiply_pass(
                            h_acc[m], (x_codes, x_scales), x_tokens(c, m),
                            codes[s], slice(BANK * b, BANK * (b + 1)),
                            c == 0, c == PASSES - 1,
                        )

        def multiply_tail(n, m):
            columns = slice(BANK * n, BANK * (n + 1))
            tail_logits[(n, m)] = bank(TAIL_BANK_ORDER[m][n], "tail_logits")
            multiply_pass(
                tail_logits[(n, m)], (h_codes, h_scales), slice(P * m, P * (m + 1)),
                (tail_codes, tail_scales), columns, True, True,
            )

        head_exp = stats("head_exp", HEAD)
        head_bank_max = stats("head_bank_max", HEAD_BANKS)
        head_neg_max = stats("head_neg_max", 1)
        head_bank_sum = stats("head_bank_sum", HEAD_BANKS)
        head_sum = stats("head_sum", 1)
        head_inverse = stats("head_inverse", 1)
        cluster0 = stats("cluster0_", 1)

        def max_head(m):
            for n in range(HEAD_BANKS):
                nc.vector.reduce_max(
                    out=head_bank_max[m][:, n : n + 1], in_=head_acc[m][n], axis=ALONG_ROW
                )

        def join_head_max(m):
            nc.vector.tensor_reduce(
                out=head_neg_max[m][:], in_=head_bank_max[m][:], axis=ALONG_ROW, op=MAX, negate=True
            )

        def exp_head(m):
            for n in range(HEAD_BANKS):
                nc.scalar.activation(
                    out=head_exp[m][:, BANK * n : BANK * (n + 1)],
                    in_=head_acc[m][n],
                    func=EXP,
                    bias=head_neg_max[m][:],
                    accum_out=head_bank_sum[m][:, n : n + 1],
                )

        def sum_head(m):
            nc.vector.reduce_sum(out=head_sum[m][:], in_=head_bank_sum[m][:], axis=ALONG_ROW)

        def invert_head(m):
            nc.vector.reciprocal(out=head_inverse[m][:], in_=head_sum[m][:])

        def scale_clusters(m):
            for column, target in ((0, cluster0[m][:]), (1, cluster1[:, m : m + 1])):
                nc.gpsimd.tensor_scalar(
                    out=target,
                    in0=head_exp[m][:, HEAD_TOKENS + column : HEAD_TOKENS + column + 1],
                    scalar1=head_inverse[m][:],
                    scalar2=0.0,
                    op0=MULT,
                    op1=ADD,
                )

        def scale_head(m):
            nc.gpsimd.tensor_scalar(
                out=head_exp[m][:, 0:HEAD_TOKENS],
                in0=head_exp[m][:, 0:HEAD_TOKENS],
                scalar1=head_inverse[m][:],
                scalar2=0.0,
                op0=MULT,
                op1=ADD,
            )

        def store_head(m):
            nc.sync.dma_start(out=out_0[m, :, 0:HEAD_TOKENS], in_=head_exp[m][:, 0:HEAD_TOKENS])

        cluster1_rows = []
        cluster1_out = keep.tile([P, P], F32, name="cluster1_out")

        def turn_cluster1():
            rows = bank(4, "cluster1_rows")
            nc.tensor.transpose(rows[:, 0:P], cluster1[:], identity[:])
            cluster1_rows.append(rows)

        def copy_cluster1():
            nc.scalar.copy(out=cluster1_out[:], in_=cluster1_rows[0][:, 0:P])

        def store_cluster1():
            nc.sync.dma_start(
                out=out_1.rearrange("n t o -> n (t o)"), in_=cluster1_out[0:TOKEN_TILES, :]
            )

        h_rounded = [keep.tile([P, PROJ], BF16, name="h_rounded%d" % m) for m in range(TOKEN_TILES)]
        h_grouped = keep.tile([P, TOKENS * PACK], BF16, align_bytes=64, name="h_grouped")
        h_codes = keep.tile([P, TOKENS], U32, align_bytes=64, name="h_codes")
        h_scales = keep.tile([P, TOKENS], U8, align_bytes=64, name="h_scales")
        h_transposed = []

        def round_h():
            for m in range(TOKEN_TILES):
                nc.scalar.copy(out=h_rounded[m][:], in_=h_acc[m])

        def transpose_h():
            h_transposed.append(bank(6, "ht").rearrange("p (u r) -> p u r", u=2))
            words = [
                h_rounded[m][:].bitcast(F32).rearrange("r (p u) -> r u p", u=2)
                for m in range(TOKEN_TILES)
            ]
            transpose_rows(words, h_transposed[0])

        def copy_h():
            nc.scalar.copy(
                out=h_grouped[:].bitcast(F32).rearrange("p (r u) -> p r u", u=2),
                in_=h_transposed[0].rearrange("p u r -> p r u"),
            )

        def quantise_h():
            nc.vector.quantize_mx(
                out=h_codes[:].bitcast(FP8X4), scales=h_scales[:], in_=h_grouped[:]
            )

        LAST = TAIL_BANKS - 1
        tail_exp = stats("tail_exp", TAIL)
        bank_neg_max = stats("bank_neg_max", TAIL_BANKS)
        bank_sum = stats("bank_sum", TAIL_BANKS)
        tail_neg_max = stats("tail_neg_max", 1)
        factor = stats("factor", TAIL_BANKS)
        cluster_factor = stats("cluster_factor", TAIL_BANKS)
        scaled_sum = stats("scaled_sum", LAST)
        early_sum = stats("early_sum", 1)
        tail_sum = stats("tail_sum", 1)
        tail_inverse = stats("tail_inverse", 1)

        def max_bank(n, m):
            nc.vector.tensor_reduce(
                out=bank_neg_max[m][:, n : n + 1],
                in_=tail_logits[(n, m)],
                axis=ALONG_ROW,
                op=MAX,
                negate=True,
            )

        def exp_bank(n, m):
            nc.scalar.activation(
                out=tail_exp[m][:, BANK * n : BANK * (n + 1)],
                in_=tail_logits[(n, m)],
                func=EXP,
                bias=bank_neg_max[m][:, n : n + 1],
                accum_out=bank_sum[m][:, n : n + 1],
            )

        def join_tail_max(m):
            nc.vector.tensor_reduce(
                out=tail_neg_max[m][:], in_=bank_neg_max[m][:], axis=ALONG_ROW, op=MIN
            )

        def exp_factor(m):
            nc.scalar.activation(
                out=factor[m][:],
                in_=bank_neg_max[m][:],
                func=EXP,
                scale=-1.0,
                bias=tail_neg_max[m][:],
            )

        def scale_factor(m):
            nc.vector.tensor_scalar(
                out=cluster_factor[m][:], in0=factor[m][:], scalar1=cluster0[m][:], scalar2=None, op0=MULT
            )

        def scale_sums(m):
            nc.vector.tensor_tensor(
                out=scaled_sum[m][:], in0=factor[m][:, 0:LAST], in1=bank_sum[m][:, 0:LAST], op=MULT
            )

        def add_sums(m):
            nc.vector.reduce_sum(out=early_sum[m][:], in_=scaled_sum[m][:], axis=ALONG_ROW)

        def join_sums(m):
            nc.vector.scalar_tensor_tensor(
                out=tail_sum[m][:],
                in0=bank_sum[m][:, LAST:TAIL_BANKS],
                scalar=factor[m][:, LAST:TAIL_BANKS],
                in1=early_sum[m][:],
                op0=MULT,
                op1=ADD,
            )

        def invert_tail(m):
            nc.vector.reciprocal(out=tail_inverse[m][:], in_=tail_sum[m][:])

        def scale_bank(n, m):
            columns = slice(BANK * n, BANK * (n + 1))
            nc.vector.tensor_scalar(
                out=tail_exp[m][:, columns],
                in0=tail_exp[m][:, columns],
                scalar1=cluster_factor[m][:, n : n + 1],
                scalar2=tail_inverse[m][:],
                op0=MULT,
                op1=MULT,
            )
            nc.sync.dma_start(
                out=out_0[m, :, HEAD_TOKENS + BANK * n : HEAD_TOKENS + BANK * (n + 1)],
                in_=tail_exp[m][:, columns],
            )

        x_transposed_in = {
            s + 1 + i: [X_GROUP * g + i] for g, s in enumerate(PROJ_STEPS) for i in range(X_GROUP)
        }
        x_transposed_in[PROJ_STEPS[0] + 1] = []
        x_transposed_in[PROJ_STEPS[0] + 2] = [0, 1]
        x_transposed_in[PROJ_STEPS[1] + 2] = [2, 3]
        x_quantised_in = {s + 1 + X_GROUP: g for g, s in enumerate(PROJ_STEPS)}
        multiplied_in = {s: [s - 4] for s in range(4, FIRST_TAIL - 1)}
        multiplied_in[FIRST_TAIL - 1] = [FIRST_TAIL - 5, FIRST_TAIL - 4]
        multiplied_in[FIRST_TAIL] = [FIRST_TAIL - 3, FIRST_TAIL - 2]
        multiplied_in[FIRST_TAIL + 1] = [FIRST_TAIL - 1]

        identity_matmuls(0)
        for s in range(STEPS):
            load(s + PREFETCH)
            if s == FIRST_TAIL:
                round_h()
                transpose_h()
            regroup(s, SCALAR)
            regroup(s, TENSOR)
            for c in x_transposed_in.get(s, []):
                transpose_x(c)
                copy_x(c)
            if s == FIRST_TAIL:
                copy_h()
            if 0 < s < EARLY_STEPS:
                quantise(s - 1)
            regroup(s, VECTOR)
            if s == FIRST_TAIL + 1:
                quantise_h()
            if s in x_quantised_in:
                quantise_x(x_quantised_in[s])
            if s >= EARLY_STEPS:
                quantise(s - 1)
            for job in multiplied_in.get(s, []):
                multiply(job)
            if s + 1 < STEPS:
                identity_matmuls(s + 1)
            if s == STEPS - 2:
                multiply_tail(0, 0)
                max_head(0)
            if s == STEPS - 1:
                join_head_max(0)
                exp_head(0)
                max_head(1)
        quantise(STEPS - 1)
        join_head_max(1)
        exp_head(1)
        for n in range(1, TAIL_BANKS):
            multiply_tail(n, 0)
        max_bank(0, 0)
        exp_bank(0, 0)
        sum_head(0)
        max_bank(1, 0)
        exp_bank(1, 0)
        invert_head(0)
        sum_head(1)
        max_bank(2, 0)
        exp_bank(2, 0)
        invert_head(1)
        scale_clusters(0)
        scale_head(0)
        store_head(0)
        max_bank(3, 0)
        exp_bank(3, 0)
        scale_clusters(1)
        scale_head(1)
        store_head(1)
        join_tail_max(0)
        exp_factor(0)
        for n in range(TAIL_BANKS):
            multiply_tail(n, 1)
        max_bank(0, 1)
        scale_sums(0)
        scale_factor(0)
        exp_bank(0, 1)
        add_sums(0)
        max_bank(1, 1)
        exp_bank(1, 1)
        join_sums(0)
        turn_cluster1()
        max_bank(2, 1)
        exp_bank(2, 1)
        invert_tail(0)
        max_bank(3, 1)
        scale_bank(0, 0)
        join_tail_max(1)
        exp_factor(1)
        exp_bank(3, 1)
        copy_cluster1()
        scale_bank(1, 0)
        scale_bank(2, 0)
        scale_sums(1)
        scale_factor(1)
        scale_bank(3, 0)
        add_sums(1)
        join_sums(1)
        invert_tail(1)
        for n in range(TAIL_BANKS):
            scale_bank(n, 1)
        store_cluster1()
